import numpy as np
import ml_dtypes


def mxq(x, axis, fmt="e4m3"):
    dtype, down = {"e4m3": (ml_dtypes.float8_e4m3fn, 7), "e5m2": (ml_dtypes.float8_e5m2, 14)}[fmt]
    v = np.moveaxis(np.asarray(x, np.float32).astype(ml_dtypes.bfloat16).astype(np.float64), axis, -1)
    blocks = v.reshape(v.shape[:-1] + (-1, 32))
    amax = np.abs(blocks).max(-1, keepdims=True)
    byte = np.maximum(np.where(amax > 0, np.frexp(amax)[1] - 1 + 127, 0) - down, 1)
    scale = np.exp2(byte - 127.0)
    codes = (blocks / scale).astype(np.float32).astype(dtype).astype(np.float64)
    return np.moveaxis((codes * scale).reshape(v.shape), -1, axis)


WIDE = False


def mx_kscale(k):
    if not WIDE:
        return np.ones(k)
    levels = np.array([10, -10, 5, -5, 0])
    a = np.random.permutation(np.resize(levels, k // 512 * 4)).reshape(k // 512, 4)
    idx = np.arange(k)
    return np.exp2(a[idx // 512, idx % 128 // 32])


BF16 = ml_dtypes.bfloat16


def bf(x):
    return np.asarray(x, np.float32).astype(BF16)


def f64(x):
    return np.asarray(x).astype(np.float64)


B, C, H, W, DM, GH = 8, 512, 32, 32, 128, 1024
OFFSETS = [(-4, -4), (-4, -1), (-4, 2), (-3, 4), (-2, -3), (2, 3), (3, -2), (4, 4)]
N = len(OFFSETS)


def setup_inputs():
    s = mx_kscale(C)
    e = np.exp(0.7 * np.random.standard_normal((N, B)))
    return {'x': bf(np.random.standard_normal((B, C, H, W)) * s[None, :, None, None]),
            'mw': bf(np.random.standard_normal((C, C)) * 2.0 / np.sqrt(C) / s[None, :]),
            'mb': bf(np.random.standard_normal(C) * 0.3),
            'attn_w': bf(e / e.sum(0, keepdims=True))}


def reference(x, mw, mb, attn_w):
    xq = mxq(f64(x).reshape(B, C, H * W), 1, 'e4m3')
    m = (mxq(f64(mw), 1, 'e4m3') @ xq).reshape(B, C, H, W) + f64(mb)[None, :, None, None]
    wts = f64(attn_w)
    agg = np.zeros_like(m)
    for i, (dy, dx) in enumerate(OFFSETS):
        agg = agg + np.roll(m, (dy, dx), axis=(2, 3)) * wts[i][:, None, None, None]
    return agg

@@ -1,0 +1,212 @@
+import concourse.mybir as mybir
+from concourse.masks import make_identity
+
+F32 = mybir.dt.float32
+BF16 = mybir.dt.bfloat16
+U32 = mybir.dt.uint32
+U8 = mybir.dt.uint8
+FP8X4 = mybir.dt.float8_e4m3fn_x4
+MULT = mybir.AluOpType.mult
+ADD = mybir.AluOpType.add
+IDENTITY = mybir.ActivationFunctionType.Identity
+
+B, C, H, W = 8, 512, 32, 32
+OFFSETS = [(-4, -4), (-4, -1), (-4, 2), (-3, 4), (-2, -3), (2, 3), (3, -2), (4, 4)]
+TAPS = len(OFFSETS)
+FLOPS = 2 * B * C * C * H * W + 2 * TAPS * B * C * H * W
+
+P = 128
+PACK = 4
+D_TILES = C // P
+PAIR = 2
+
+PAD = 4
+PITCH = W + 2 * PAD
+ROW0 = 2
+BAND = 8
+BANDS = H // BAND
+BANK_COLS = 512
+BANK_ROWS = BANK_COLS // PITCH
+ROWS = (BANDS - 1) * BAND + BANK_ROWS
+WORDS = 1536
+QUANT_WIDTHS = (4096, 2048)
+REGROUP_ROWS = 6
+REGROUP_STEPS = ROWS // REGROUP_ROWS
+
+
+def tap_window(dy, dx):
+    bank_step, first_row = divmod(-dy - ROW0, BAND)
+    assert bank_step in (-1, 0) and first_row + BAND <= BANK_ROWS
+    return bank_step, first_row, PAD - dx
+
+
+def tile_graphaugmentation_pa_t_kernel(tc, x, mw, mb, attn_w, out):
+    nc = tc.nc
+    with tc.manual_schedule(), tc.tile_pool(name="const", bufs=1) as const, tc.tile_pool(
+        name="raws", bufs=B
+    ) as raws, tc.tile_pool(name="accs", bufs=3) as accs:
+        mw_sb = const.tile([P, D_TILES * C], BF16, name="mw_sb")
+        nc.sync.dma_start(
+            out=mw_sb.rearrange("p (t c) -> p t c", t=D_TILES),
+            in_=mw.rearrange("(t p) c -> p t c", p=P),
+        )
+        raw_tiles = []
+        for b in range(B):
+            raw = raws.tile([P, PACK, ROWS * W], BF16, name="raw")
+            xb = x[b].rearrange("(p t) h w -> p t (h w)", t=PACK)
+            first = (H - ROW0) * W
+            nc.sync.dma_start(out=raw[:, :, 0:first], in_=xb[:, :, ROW0 * W : H * W])
+            nc.sync.dma_start(out=raw[:, :, first : ROWS * W], in_=xb[:, :, 0 : ROWS * W - first])
+            raw_tiles.append(raw)
+
+        w_bf = const.tile([P, TAPS * B], BF16, name="w_bf")
+        nc.scalar.dma_start(out=w_bf[:], in_=attn_w.rearrange("i b -> (i b)").partition_broadcast(P))
+        mb_rows = const.tile([P, P], BF16, name="mb_rows")
+        nc.vector.memset(mb_rows[:], 0.0)
+        nc.scalar.dma_start(out=mb_rows[0:D_TILES, :], in_=mb.rearrange("(t p) -> t p", p=P))
+
+        ident = const.tile([P, P], F32, name="ident")
+        make_identity(nc, ident[:])
+
+        mw_words32 = mw_sb[:].bitcast(F32)
+        half_c = C // 2
+        mw_grouped = const.tile([P, C * PACK], BF16, name="mw_grouped", align_bytes=64)
+        mw_grouped32 = mw_grouped[:].bitcast(F32).rearrange("p (t d u) -> p t d u", t=D_TILES, u=2)
+        mw_codes = const.tile([P, C], U32, name="mw_codes", align_bytes=64)
+        mw_scales = const.tile([P, C], U8, name="mw_scales", align_bytes=64)
+        mb_col = const.tile([P, D_TILES], F32, name="mb_col")
+        with tc.psum_pool(name="prep", bufs=1) as prep:
+            for pair in range(D_TILES // PAIR):
+                mw_t = prep.tile([P, PAIR, 2, P], F32, name="mw_t%d" % pair)
+                for s in range(PAIR):
+                    t = pair * PAIR + s
+                    for u in range(2):
+                        nc.tensor.transpose(
+                            mw_t[:, s, u, :],
+                            mw_words32[:, t * half_c + u : (t + 1) * half_c : 2],
+                            ident[:],
+                        )
+                nc.vector.tensor_copy(
+                    out=mw_grouped32[:, pair * PAIR : (pair + 1) * PAIR],
+                    in_=mw_t.rearrange("p s u d -> p s d u"),
+                )
+            nc.vector.quantize_mx(
+                out=mw_codes[:].bitcast(FP8X4), scales=mw_scales[:], in_=mw_grouped[:]
+            )
+            mb_rows32 = const.tile([P, P], F32, name="mb_rows32")
+            nc.vector.tensor_copy(out=mb_rows32[:], in_=mb_rows[:])
+            mb_t = prep.tile([P, P], F32, name="mb_t")
+            nc.tensor.transpose(mb_t[:], mb_rows32[:], ident[:])
+            nc.vector.tensor_copy(out=mb_col[:], in_=mb_t[:, 0:D_TILES])
+
+        weight = const.tile([P, TAPS * B], F32, name="weight")
+        nc.vector.tensor_copy(out=weight[:], in_=w_bf[:])
+        weight_sum = const.tile([P, B], F32, name="weight_sum")
+        nc.vector.tensor_reduce(
+            out=weight_sum[:],
+            in_=weight[:].rearrange("p (i b) -> p b i", b=B),
+            axis=mybir.AxisListType.X,
+            op=ADD,
+        )
+        bias = const.tile([P, D_TILES * B], F32, name="bias")
+        for t in range(D_TILES):
+            nc.vector.tensor_scalar_mul(
+                out=bias[:, t * B : (t + 1) * B], in0=weight_sum[:], scalar1=mb_col[:, t : t + 1]
+            )
+
+        grouped = const.tile([P, WORDS * PACK], BF16, name="grouped", align_bytes=64)
+        nc.vector.memset(grouped[:, ROWS * PITCH * PACK :], 0.0)
+        grouped_rows = grouped[:, 0 : ROWS * PITCH * PACK].rearrange(
+            "p (r c t) -> p r c t", c=PITCH, t=PACK
+        )
+        x_codes = [const.tile([P, WORDS], U32, name="x_codes%d" % s, align_bytes=64) for s in range(2)]
+        x_scales = [const.tile([P, WORDS], U8, name="x_scales%d" % s, align_bytes=64) for s in range(2)]
+
+        def regroup(b, step):
+            rows = slice(step * REGROUP_ROWS, (step + 1) * REGROUP_ROWS)
+            src = raw_tiles[b].rearrange("p t (r w) -> p r w t", w=W)
+            nc.scalar.copy(out=grouped_rows[:, rows, PAD : PAD + W, :], in_=src[:, rows, :, :])
+            nc.scalar.copy(out=grouped_rows[:, rows, 0:PAD, :], in_=src[:, rows, W - PAD : W, :])
+            nc.scalar.copy(out=grouped_rows[:, rows, PAD + W : PITCH, :], in_=src[:, rows, 0:PAD, :])
+
+        def quantise(b):
+            start = 0
+            for width in QUANT_WIDTHS:
+                words = slice(start // PACK, (start + width) // PACK)
+                nc.vector.quantize_mx(
+                    out=x_codes[b % 2][:, words].bitcast(FP8X4),
+                    scales=x_scales[b % 2][:, words],
+                    in_=grouped[:, start : start + width],
+                )
+                start += width
+
+        for step in range(REGROUP_STEPS):
+            regroup(0, step)
+        quantise(0)
+
+        with tc.psum_pool(name="banks", bufs=8) as banks:
+
+            def fill(b, t, k):
+                bank = banks.tile([P, BANK_COLS], F32, name="bank")
+                d_cols = slice(t * P, (t + 1) * P)
+                words = slice(k * BAND * PITCH, k * BAND * PITCH + BANK_COLS)
+                nc.tensor.matmul_mx(
+                    out=bank[:],
+                    lhsT=mw_codes[:, d_cols].bitcast(FP8X4),
+                    lhsT_scale=mw_scales[:, d_cols],
+                    rhs=x_codes[b % 2][:, words].bitcast(FP8X4),
+                    rhs_scale=x_scales[b % 2][:, words],
+                    start=True,
+                    stop=True,
+                )
+                return bank[:, 0 : BANK_ROWS * PITCH].rearrange("p (r c) -> p r c", c=PITCH)
+
+            for b in range(B):
+                for pair in range(D_TILES // PAIR):
+                    acc = accs.tile([P, PAIR, H * W], F32, name="acc")
+                    d_tiles = [pair * PAIR + s for s in range(PAIR)]
+                    before = [fill(b, t, BANDS - 1) for t in d_tiles]
+                    for j in range(BANDS):
+                        here = [fill(b, t, j) for t in d_tiles]
+                        bands = [
+                            acc[:, s, j * BAND * W : (j + 1) * BAND * W].rearrange(
+                                "p (r c) -> p r c", c=W
+                            )
+                            for s in range(PAIR)
+                        ]
+                        for i, (dy, dx) in enumerate(OFFSETS):
+                            bank_step, row, col = tap_window(dy, dx)
+                            w_i = weight[:, i * B + b : i * B + b + 1]
+                            for s in range(PAIR):
+                                source = (here if bank_step == 0 else before)[s]
+                                window = source[:, row : row + BAND, col : col + W]
+                                if i == 0:
+                                    t = d_tiles[s]
+                                    nc.scalar.activation(
+                                        out=bands[s],
+                                        in_=window,
+                                        func=IDENTITY,
+                                        bias=bias[:, t * B + b : t * B + b + 1],
+                                        scale=w_i,
+                                    )
+                                else:
+                                    nc.vector.scalar_tensor_tensor(
+                                        out=bands[s],
+                                        in0=window,
+                                        scalar=w_i,
+                                        in1=bands[s],
+                                        op0=MULT,
+                                        op1=ADD,
+                                    )
+                        before = here
+                        step = pair * BANDS + j
+                        if b + 1 < B and step < REGROUP_STEPS:
+                            regroup(b + 1, step)
+                        if b + 1 < B and step == REGROUP_STEPS:
+                            quantise(b + 1)
+                    nc.sync.dma_start(
+                        out=out[b, pair * PAIR * P : (pair + 1) * PAIR * P].rearrange(
+                            "(s p) h w -> p s (h w)", p=P
+                        ),
+                        in_=acc[:],
+                    )

@@ -32,6 +32,8 @@ WORDS = 1536
 QUANT_WIDTHS = (4096, 2048)
 REGROUP_ROWS = 6
 REGROUP_STEPS = ROWS // REGROUP_ROWS
+BAND_ORDER = [(n + 1) % BANDS for n in range(BANDS)]
+SCALAR_TAPS = 3
 
 
 def tap_window(dy, dx):
@@ -44,7 +46,7 @@ def tile_graphaugmentation_pa_t_kernel(tc, x, mw, mb, attn_w, out):
     nc = tc.nc
     with tc.manual_schedule(), tc.tile_pool(name="const", bufs=1) as const, tc.tile_pool(
         name="raws", bufs=B
-    ) as raws, tc.tile_pool(name="accs", bufs=3) as accs:
+    ) as raws, tc.tile_pool(name="accs", bufs=3) as accs, tc.tile_pool(name="sides", bufs=2) as sides:
         mw_sb = const.tile([P, D_TILES * C], BF16, name="mw_sb")
         nc.sync.dma_start(
             out=mw_sb.rearrange("p (t c) -> p t c", t=D_TILES),
@@ -122,12 +124,12 @@ def tile_graphaugmentation_pa_t_kernel(tc, x, mw, mb, attn_w, out):
         x_codes = [const.tile([P, WORDS], U32, name="x_codes%d" % s, align_bytes=64) for s in range(2)]
         x_scales = [const.tile([P, WORDS], U8, name="x_scales%d" % s, align_bytes=64) for s in range(2)]
 
-        def regroup(b, step):
+        def regroup(copy, b, step):
             rows = slice(step * REGROUP_ROWS, (step + 1) * REGROUP_ROWS)
             src = raw_tiles[b].rearrange("p t (r w) -> p r w t", w=W)
-            nc.scalar.copy(out=grouped_rows[:, rows, PAD : PAD + W, :], in_=src[:, rows, :, :])
-            nc.scalar.copy(out=grouped_rows[:, rows, 0:PAD, :], in_=src[:, rows, W - PAD : W, :])
-            nc.scalar.copy(out=grouped_rows[:, rows, PAD + W : PITCH, :], in_=src[:, rows, 0:PAD, :])
+            copy(out=grouped_rows[:, rows, PAD : PAD + W, :], in_=src[:, rows, :, :])
+            copy(out=grouped_rows[:, rows, 0:PAD, :], in_=src[:, rows, W - PAD : W, :])
+            copy(out=grouped_rows[:, rows, PAD + W : PITCH, :], in_=src[:, rows, 0:PAD, :])
 
         def quantise(b):
             start = 0
@@ -141,7 +143,7 @@ def tile_graphaugmentation_pa_t_kernel(tc, x, mw, mb, attn_w, out):
                 start += width
 
         for step in range(REGROUP_STEPS):
-            regroup(0, step)
+            regroup(nc.scalar.copy if step % 3 == 2 else nc.vector.tensor_copy, 0, step)
         quantise(0)
 
         with tc.psum_pool(name="banks", bufs=8) as banks:
@@ -164,46 +166,47 @@ def tile_graphaugmentation_pa_t_kernel(tc, x, mw, mb, attn_w, out):
             for b in range(B):
                 for pair in range(D_TILES // PAIR):
                     acc = accs.tile([P, PAIR, H * W], F32, name="acc")
+                    side_a = sides.tile([P, PAIR, H * W], F32, name="side_a")
+                    side_b = sides.tile([P, PAIR, H * W], F32, name="side_b")
+                    products = [acc, side_a, side_b]
                     d_tiles = [pair * PAIR + s for s in range(PAIR)]
-                    before = [fill(b, t, BANDS - 1) for t in d_tiles]
-                    for j in range(BANDS):
+                    before = [fill(b, t, BAND_ORDER[0] - 1) for t in d_tiles]
+                    for n, j in enumerate(BAND_ORDER):
                         here = [fill(b, t, j) for t in d_tiles]
-                        bands = [
-                            acc[:, s, j * BAND * W : (j + 1) * BAND * W].rearrange(
-                                "p (r c) -> p r c", c=W
-                            )
-                            for s in range(PAIR)
-                        ]
-                        for i, (dy, dx) in enumerate(OFFSETS):
-                            bank_step, row, col = tap_window(dy, dx)
-                            w_i = weight[:, i * B + b : i * B + b + 1]
+                        pixels = slice(j * BAND * W, (j + 1) * BAND * W)
+                        for i in reversed(range(SCALAR_TAPS)):
+                            bank_step, row, col = tap_window(*OFFSETS[i])
+                            assert bank_step == 0
+                            for s in range(PAIR):
+                                column = d_tiles[s] * B + b
+                                nc.scalar.activation(
+                                    out=products[i][:, s, pixels].rearrange("p (r c) -> p r c", c=W),
+                                    in_=here[s][:, row : row + BAND, col : col + W],
+                                    func=IDENTITY,
+                                    bias=bias[:, column : column + 1] if i == 0 else 0.0,
+                                    scale=weight[:, i * B + b : i * B + b + 1],
+                                )
+                        for i in range(SCALAR_TAPS, TAPS):
+                            bank_step, row, col = tap_window(*OFFSETS[i])
                             for s in range(PAIR):
                                 source = (here if bank_step == 0 else before)[s]
-                                window = source[:, row : row + BAND, col : col + W]
-                                if i == 0:
-                                    t = d_tiles[s]
-                                    nc.scalar.activation(
-                                        out=bands[s],
-                                        in_=window,
-                                        func=IDENTITY,
-                                        bias=bias[:, t * B + b : t * B + b + 1],
-                                        scale=w_i,
-                                    )
-                                else:
-                                    nc.vector.scalar_tensor_tensor(
-                                        out=bands[s],
-                                        in0=window,
-                                        scalar=w_i,
-                                        in1=bands[s],
-                                        op0=MULT,
-                                        op1=ADD,
-                                    )
+                                band = acc[:, s, pixels].rearrange("p (r c) -> p r c", c=W)
+                                nc.vector.scalar_tensor_tensor(
+                                    out=band,
+                                    in0=source[:, row : row + BAND, col : col + W],
+                                    scalar=weight[:, i * B + b : i * B + b + 1],
+                                    in1=band,
+                                    op0=MULT,
+                                    op1=ADD,
+                                )
                         before = here
-                        step = pair * BANDS + j
+                        step = pair * BANDS + n
                         if b + 1 < B and step < REGROUP_STEPS:
-                            regroup(b + 1, step)
+                            regroup(nc.scalar.copy, b + 1, step)
                         if b + 1 < B and step == REGROUP_STEPS:
                             quantise(b + 1)
+                    nc.gpsimd.tensor_tensor(out=side_a[:], in0=side_a[:], in1=side_b[:], op=ADD)
+                    nc.gpsimd.tensor_tensor(out=acc[:], in0=acc[:], in1=side_a[:], op=ADD)
                     nc.sync.dma_start(
                         out=out[b, pair * PAIR * P : (pair + 1) * PAIR * P].rearrange(
                             "(s p) h w -> p s (h w)", p=P

@@ -48,10 +48,6 @@ def tile_graphaugmentation_pa_t_kernel(tc, x, mw, mb, attn_w, out):
         name="raws", bufs=B
     ) as raws, tc.tile_pool(name="accs", bufs=3) as accs, tc.tile_pool(name="sides", bufs=2) as sides:
         mw_sb = const.tile([P, D_TILES * C], BF16, name="mw_sb")
-        nc.sync.dma_start(
-            out=mw_sb.rearrange("p (t c) -> p t c", t=D_TILES),
-            in_=mw.rearrange("(t p) c -> p t c", p=P),
-        )
         raw_tiles = []
         for b in range(B):
             raw = raws.tile([P, PACK, ROWS * W], BF16, name="raw")
@@ -60,6 +56,11 @@ def tile_graphaugmentation_pa_t_kernel(tc, x, mw, mb, attn_w, out):
             nc.sync.dma_start(out=raw[:, :, 0:first], in_=xb[:, :, ROW0 * W : H * W])
             nc.sync.dma_start(out=raw[:, :, first : ROWS * W], in_=xb[:, :, 0 : ROWS * W - first])
             raw_tiles.append(raw)
+            if b == 0:
+                nc.sync.dma_start(
+                    out=mw_sb.rearrange("p (t c) -> p t c", t=D_TILES),
+                    in_=mw.rearrange("(t p) c -> p t c", p=P),
+                )
 
         w_bf = const.tile([P, TAPS * B], BF16, name="w_bf")
         nc.scalar.dma_start(out=w_bf[:], in_=attn_w.rearrange("i b -> (i b)").partition_broadcast(P))
@@ -69,52 +70,6 @@ def tile_graphaugmentation_pa_t_kernel(tc, x, mw, mb, attn_w, out):
 
         ident = const.tile([P, P], F32, name="ident")
         make_identity(nc, ident[:])
-
-        mw_words32 = mw_sb[:].bitcast(F32)
-        half_c = C // 2
-        mw_grouped = const.tile([P, C * PACK], BF16, name="mw_grouped", align_bytes=64)
-        mw_grouped32 = mw_grouped[:].bitcast(F32).rearrange("p (t d u) -> p t d u", t=D_TILES, u=2)
-        mw_codes = const.tile([P, C], U32, name="mw_codes", align_bytes=64)
-        mw_scales = const.tile([P, C], U8, name="mw_scales", align_bytes=64)
-        mb_col = const.tile([P, D_TILES], F32, name="mb_col")
-        with tc.psum_pool(name="prep", bufs=1) as prep:
-            for pair in range(D_TILES // PAIR):
-                mw_t = prep.tile([P, PAIR, 2, P], F32, name="mw_t%d" % pair)
-                for s in range(PAIR):
-                    t = pair * PAIR + s
-                    for u in range(2):
-                        nc.tensor.transpose(
-                            mw_t[:, s, u, :],
-                            mw_words32[:, t * half_c + u : (t + 1) * half_c : 2],
-                            ident[:],
-                        )
-                nc.vector.tensor_copy(
-                    out=mw_grouped32[:, pair * PAIR : (pair + 1) * PAIR],
-                    in_=mw_t.rearrange("p s u d -> p s d u"),
-                )
-            nc.vector.quantize_mx(
-                out=mw_codes[:].bitcast(FP8X4), scales=mw_scales[:], in_=mw_grouped[:]
-            )
-            mb_rows32 = const.tile([P, P], F32, name="mb_rows32")
-            nc.vector.tensor_copy(out=mb_rows32[:], in_=mb_rows[:])
-            mb_t = prep.tile([P, P], F32, name="mb_t")
-            nc.tensor.transpose(mb_t[:], mb_rows32[:], ident[:])
-            nc.vector.tensor_copy(out=mb_col[:], in_=mb_t[:, 0:D_TILES])
-
-        weight = const.tile([P, TAPS * B], F32, name="weight")
-        nc.vector.tensor_copy(out=weight[:], in_=w_bf[:])
-        weight_sum = const.tile([P, B], F32, name="weight_sum")
-        nc.vector.tensor_reduce(
-            out=weight_sum[:],
-            in_=weight[:].rearrange("p (i b) -> p b i", b=B),
-            axis=mybir.AxisListType.X,
-            op=ADD,
-        )
-        bias = const.tile([P, D_TILES * B], F32, name="bias")
-        for t in range(D_TILES):
-            nc.vector.tensor_scalar_mul(
-                out=bias[:, t * B : (t + 1) * B], in0=weight_sum[:], scalar1=mb_col[:, t : t + 1]
-            )
 
         grouped = const.tile([P, WORDS * PACK], BF16, name="grouped", align_bytes=64)
         nc.vector.memset(grouped[:, ROWS * PITCH * PACK :], 0.0)
@@ -142,9 +97,56 @@ def tile_graphaugmentation_pa_t_kernel(tc, x, mw, mb, attn_w, out):
                 )
                 start += width
 
-        for step in range(REGROUP_STEPS):
-            regroup(nc.scalar.copy if step % 3 == 2 else nc.vector.tensor_copy, 0, step)
-        quantise(0)
+        weight = const.tile([P, TAPS * B], F32, name="weight")
+        nc.vector.tensor_copy(out=weight[:], in_=w_bf[:])
+        weight_sum = const.tile([P, B], F32, name="weight_sum")
+        nc.vector.tensor_reduce(
+            out=weight_sum[:],
+            in_=weight[:].rearrange("p (i b) -> p b i", b=B),
+            axis=mybir.AxisListType.X,
+            op=ADD,
+        )
+        mb_rows32 = const.tile([P, P], F32, name="mb_rows32")
+        nc.vector.tensor_copy(out=mb_rows32[:], in_=mb_rows[:])
+        mb_col = const.tile([P, D_TILES], F32, name="mb_col")
+        bias = const.tile([P, D_TILES * B], F32, name="bias")
+
+        mw_words32 = mw_sb[:].bitcast(F32)
+        half_c = C // 2
+        mw_grouped = const.tile([P, C * PACK], BF16, name="mw_grouped", align_bytes=64)
+        mw_grouped32 = mw_grouped[:].bitcast(F32).rearrange("p (t d u) -> p t d u", t=D_TILES, u=2)
+        mw_codes = const.tile([P, C], U32, name="mw_codes", align_bytes=64)
+        mw_scales = const.tile([P, C], U8, name="mw_scales", align_bytes=64)
+        with tc.psum_pool(name="prep", bufs=1) as prep:
+            mb_t = prep.tile([P, P], F32, name="mb_t")
+            nc.tensor.transpose(mb_t[:], mb_rows32[:], ident[:])
+            nc.vector.tensor_copy(out=mb_col[:], in_=mb_t[:, 0:D_TILES])
+            for t in range(D_TILES):
+                nc.vector.tensor_scalar_mul(
+                    out=bias[:, t * B : (t + 1) * B], in0=weight_sum[:], scalar1=mb_col[:, t : t + 1]
+                )
+
+            for step in range(REGROUP_STEPS):
+                regroup(nc.scalar.copy if step % 3 == 2 else nc.vector.tensor_copy, 0, step)
+
+            for pair in range(D_TILES // PAIR):
+                mw_t = prep.tile([P, PAIR, 2, P], F32, name="mw_t%d" % pair)
+                for s in range(PAIR):
+                    t = pair * PAIR + s
+                    for u in range(2):
+                        nc.tensor.transpose(
+                            mw_t[:, s, u, :],
+                            mw_words32[:, t * half_c + u : (t + 1) * half_c : 2],
+                            ident[:],
+                        )
+                nc.vector.tensor_copy(
+                    out=mw_grouped32[:, pair * PAIR : (pair + 1) * PAIR],
+                    in_=mw_t.rearrange("p s u d -> p s d u"),
+                )
+            nc.vector.quantize_mx(
+                out=mw_codes[:].bitcast(FP8X4), scales=mw_scales[:], in_=mw_grouped[:]
+            )
+            quantise(0)
 
         with tc.psum_pool(name="banks", bufs=8) as banks:
 
@@ -200,16 +202,20 @@ def tile_graphaugmentation_pa_t_kernel(tc, x, mw, mb, attn_w, out):
                                     op1=ADD,
                                 )
                         before = here
+                        nc.gpsimd.tensor_tensor(
+                            out=side_a[:, :, pixels], in0=side_a[:, :, pixels], in1=side_b[:, :, pixels], op=ADD
+                        )
+                        nc.gpsimd.tensor_tensor(
+                            out=acc[:, :, pixels], in0=acc[:, :, pixels], in1=side_a[:, :, pixels], op=ADD
+                        )
+                        nc.sync.dma_start(
+                            out=out[
+                                b, pair * PAIR * P : (pair + 1) * PAIR * P, j * BAND : (j + 1) * BAND, :
+                            ].rearrange("(s p) r w -> p s (r w)", p=P),
+                            in_=acc[:, :, pixels],
+                        )
                         step = pair * BANDS + n
                         if b + 1 < B and step < REGROUP_STEPS:
                             regroup(nc.scalar.copy, b + 1, step)
                         if b + 1 < B and step == REGROUP_STEPS:
                             quantise(b + 1)
-                    nc.gpsimd.tensor_tensor(out=side_a[:], in0=side_a[:], in1=side_b[:], op=ADD)
-                    nc.gpsimd.tensor_tensor(out=acc[:], in0=acc[:], in1=side_a[:], op=ADD)
-                    nc.sync.dma_start(
-                        out=out[b, pair * PAIR * P : (pair + 1) * PAIR * P].rearrange(
-                            "(s p) h w -> p s (h w)", p=P
-                        ),
-                        in_=acc[:],
-                    )

@@ -30,7 +30,7 @@ BANK_ROWS = BANK_COLS // PITCH
 ROWS = (BANDS - 1) * BAND + BANK_ROWS
 WORDS = 1536
 QUANT_WIDTHS = (4096, 2048)
-REGROUP_ROWS = 6
+REGROUP_ROWS = 9
 REGROUP_STEPS = ROWS // REGROUP_ROWS
 BAND_ORDER = [(n + 1) % BANDS for n in range(BANDS)]
 SCALAR_TAPS = 3

@@ -30,9 +30,8 @@ BANK_ROWS = BANK_COLS // PITCH
 ROWS = (BANDS - 1) * BAND + BANK_ROWS
 WORDS = 1536
 QUANT_WIDTHS = (4096, 2048)
-REGROUP_ROWS = 9
+REGROUP_ROWS = 6
 REGROUP_STEPS = ROWS // REGROUP_ROWS
-BAND_ORDER = [(n + 1) % BANDS for n in range(BANDS)]
 SCALAR_TAPS = 3
 
 
@@ -167,14 +166,13 @@ def tile_graphaugmentation_pa_t_kernel(tc, x, mw, mb, attn_w, out):
 
             for b in range(B):
                 for pair in range(D_TILES // PAIR):
+                    d_tiles = [pair * PAIR + s for s in range(PAIR)]
                     acc = accs.tile([P, PAIR, H * W], F32, name="acc")
                     side_a = sides.tile([P, PAIR, H * W], F32, name="side_a")
                     side_b = sides.tile([P, PAIR, H * W], F32, name="side_b")
                     products = [acc, side_a, side_b]
-                    d_tiles = [pair * PAIR + s for s in range(PAIR)]
-                    before = [fill(b, t, BAND_ORDER[0] - 1) for t in d_tiles]
-                    for n, j in enumerate(BAND_ORDER):
-                        here = [fill(b, t, j) for t in d_tiles]
+
+                    def scalar_products(j, banks_j):
                         pixels = slice(j * BAND * W, (j + 1) * BAND * W)
                         for i in reversed(range(SCALAR_TAPS)):
                             bank_step, row, col = tap_window(*OFFSETS[i])
@@ -183,25 +181,31 @@ def tile_graphaugmentation_pa_t_kernel(tc, x, mw, mb, attn_w, out):
                                 column = d_tiles[s] * B + b
                                 nc.scalar.activation(
                                     out=products[i][:, s, pixels].rearrange("p (r c) -> p r c", c=W),
-                                    in_=here[s][:, row : row + BAND, col : col + W],
+                                    in_=banks_j[s][:, row : row + BAND, col : col + W],
                                     func=IDENTITY,
                                     bias=bias[:, column : column + 1] if i == 0 else 0.0,
                                     scale=weight[:, i * B + b : i * B + b + 1],
                                 )
+
+                    def vector_adds(j, source, source_step):
+                        pixels = slice(j * BAND * W, (j + 1) * BAND * W)
                         for i in range(SCALAR_TAPS, TAPS):
                             bank_step, row, col = tap_window(*OFFSETS[i])
+                            if bank_step != source_step:
+                                continue
                             for s in range(PAIR):
-                                source = (here if bank_step == 0 else before)[s]
                                 band = acc[:, s, pixels].rearrange("p (r c) -> p r c", c=W)
                                 nc.vector.scalar_tensor_tensor(
                                     out=band,
-                                    in0=source[:, row : row + BAND, col : col + W],
+                                    in0=source[s][:, row : row + BAND, col : col + W],
                                     scalar=weight[:, i * B + b : i * B + b + 1],
                                     in1=band,
                                     op0=MULT,
                                     op1=ADD,
                                 )
-                        before = here
+
+                    def finish(j):
+                        pixels = slice(j * BAND * W, (j + 1) * BAND * W)
                         nc.gpsimd.tensor_tensor(
                             out=side_a[:, :, pixels], in0=side_a[:, :, pixels], in1=side_b[:, :, pixels], op=ADD
                         )
@@ -214,8 +218,21 @@ def tile_graphaugmentation_pa_t_kernel(tc, x, mw, mb, attn_w, out):
                             ].rearrange("(s p) r w -> p s (r w)", p=P),
                             in_=acc[:, :, pixels],
                         )
-                        step = pair * BANDS + n
+
+                    before = None
+                    for j in range(BANDS):
+                        here = [fill(b, t, j) for t in d_tiles]
+                        scalar_products(j, here)
+                        if j > 0:
+                            vector_adds(j, before, -1)
+                        vector_adds(j, here, 0)
+                        if j > 0:
+                            finish(j)
+                        before = here
+                        step = pair * BANDS + j
                         if b + 1 < B and step < REGROUP_STEPS:
                             regroup(nc.scalar.copy, b + 1, step)
                         if b + 1 < B and step == REGROUP_STEPS:
                             quantise(b + 1)
+                    vector_adds(0, before, -1)
+                    finish(0)

@@ -34,6 +34,11 @@ REGROUP_ROWS = 6
 REGROUP_STEPS = ROWS // REGROUP_ROWS
 SCALAR_TAPS = 3
 
+LONE = B - 1
+BLOCK_ROWS = P // W
+BLOCKS = H // BLOCK_ROWS
+BLOCK_STEPS = (-1, 0, 1)
+
 
 def tap_window(dy, dx):
     bank_step, first_row = divmod(-dy - ROW0, BAND)
@@ -44,11 +49,12 @@ def tap_window(dy, dx):
 def tile_graphaugmentation_pa_t_kernel(tc, x, mw, mb, attn_w, out):
     nc = tc.nc
     with tc.manual_schedule(), tc.tile_pool(name="const", bufs=1) as const, tc.tile_pool(
-        name="raws", bufs=B
+        name="raws", bufs=LONE
     ) as raws, tc.tile_pool(name="accs", bufs=3) as accs, tc.tile_pool(name="sides", bufs=2) as sides:
         mw_sb = const.tile([P, D_TILES * C], BF16, name="mw_sb")
         raw_tiles = []
-        for b in range(B):
+        lone_raw = const.tile([P, PACK, H * W], BF16, name="lone_raw")
+        for b in range(LONE):
             raw = raws.tile([P, PACK, ROWS * W], BF16, name="raw")
             xb = x[b].rearrange("(p t) h w -> p t (h w)", t=PACK)
             first = (H - ROW0) * W
@@ -60,6 +66,8 @@ def tile_graphaugmentation_pa_t_kernel(tc, x, mw, mb, attn_w, out):
                     out=mw_sb.rearrange("p (t c) -> p t c", t=D_TILES),
                     in_=mw.rearrange("(t p) c -> p t c", p=P),
                 )
+            if b == 1:
+                nc.sync.dma_start(out=lone_raw[:], in_=x[LONE].rearrange("(p t) h w -> p t (h w)", t=PACK))
 
         w_bf = const.tile([P, TAPS * B], BF16, name="w_bf")
         nc.scalar.dma_start(out=w_bf[:], in_=attn_w.rearrange("i b -> (i b)").partition_broadcast(P))
@@ -110,6 +118,33 @@ def tile_graphaugmentation_pa_t_kernel(tc, x, mw, mb, attn_w, out):
         mb_col = const.tile([P, D_TILES], F32, name="mb_col")
         bias = const.tile([P, D_TILES * B], F32, name="bias")
 
+        ident_rows = ident.rearrange("p (r c) -> p r c", c=W)
+        ident_wide = const.tile([P, BLOCK_ROWS, PITCH], F32, name="ident_wide")
+        nc.vector.tensor_copy(out=ident_wide[:, :, PAD : PAD + W], in_=ident_rows)
+        nc.vector.tensor_copy(out=ident_wide[:, :, 0:PAD], in_=ident_rows[:, :, W - PAD : W])
+        nc.vector.tensor_copy(out=ident_wide[:, :, PAD + W : PITCH], in_=ident_rows[:, :, 0:PAD])
+        mix = {}
+        for step in BLOCK_STEPS:
+            mix[step] = const.tile([P, BLOCK_ROWS, W], F32, name="mix%d" % (step + 1))
+            nc.vector.memset(mix[step][:], 0.0)
+        for i, (dy, dx) in enumerate(OFFSETS):
+            for step in BLOCK_STEPS:
+                shift = dy + BLOCK_ROWS * step
+                low, high = max(0, shift), min(BLOCK_ROWS, BLOCK_ROWS + shift)
+                if low < high:
+                    nc.vector.scalar_tensor_tensor(
+                        out=mix[step][:, low:high, :],
+                        in0=ident_wide[:, low - shift : high - shift, PAD - dx : PAD - dx + W],
+                        scalar=weight[:, i * B + LONE : i * B + LONE + 1],
+                        in1=mix[step][:, low:high, :],
+                        op0=MULT,
+                        op1=ADD,
+                    )
+        lone_grouped = const.tile([P, H * W * PACK], BF16, name="lone_grouped", align_bytes=64)
+        lone_codes = const.tile([P, H * W], U32, name="lone_codes", align_bytes=64)
+        lone_scales = const.tile([P, H * W], U8, name="lone_scales", align_bytes=64)
+        lone_m = const.tile([P, BLOCKS, C], F32, name="lone_m")
+
         mw_words32 = mw_sb[:].bitcast(F32)
         half_c = C // 2
         mw_grouped = const.tile([P, C * PACK], BF16, name="mw_grouped", align_bytes=64)
@@ -147,7 +182,71 @@ def tile_graphaugmentation_pa_t_kernel(tc, x, mw, mb, attn_w, out):
             )
             quantise(0)
 
-        with tc.psum_pool(name="banks", bufs=8) as banks:
+        with tc.psum_pool(name="banks", bufs=6) as banks, tc.psum_pool(name="lone_banks", bufs=2) as lone_banks, tc.tile_pool(
+            name="lone_outs", bufs=2
+        ) as lone_outs:
+
+            def lone_regroup(piece):
+                pixels = slice(piece * H * W // 4, (piece + 1) * H * W // 4)
+                nc.gpsimd.tensor_scalar(
+                    out=lone_grouped.rearrange("p (n t) -> p n t", t=PACK)[:, pixels, :],
+                    in0=lone_raw.rearrange("p t n -> p n t")[:, pixels, :],
+                    scalar1=1.0,
+                    scalar2=0.0,
+                    op0=MULT,
+                    op1=ADD,
+                )
+
+            def lone_quantise():
+                nc.vector.quantize_mx(
+                    out=lone_codes[:].bitcast(FP8X4), scales=lone_scales[:], in_=lone_grouped[:]
+                )
+
+            def lone_messages(q):
+                bank = lone_banks.tile([P, C], F32, name="lone_bank")
+                cols = slice(q * P, (q + 1) * P)
+                nc.tensor.matmul_mx(
+                    out=bank[:],
+                    lhsT=lone_codes[:, cols].bitcast(FP8X4),
+                    lhsT_scale=lone_scales[:, cols],
+                    rhs=mw_codes[:].bitcast(FP8X4),
+                    rhs_scale=mw_scales[:],
+                    start=True,
+                    stop=True,
+                )
+                nc.scalar.copy(out=lone_m[:, q, :], in_=bank[:])
+
+            lone_state = {}
+
+            def lone_sum(t, q):
+                place = q % (BANK_COLS // P)
+                if place == 0:
+                    lone_state["bank"] = lone_banks.tile([P, BANK_COLS], F32, name="lone_bank")
+                bank = lone_state["bank"]
+                for step in BLOCK_STEPS:
+                    nc.tensor.matmul(
+                        out=bank[:, place * P : (place + 1) * P],
+                        lhsT=lone_m[:, (q + step) % BLOCKS, t * P : (t + 1) * P],
+                        rhs=mix[step].rearrange("p r c -> p (r c)"),
+                        start=step == BLOCK_STEPS[0],
+                        stop=step == BLOCK_STEPS[-1],
+                    )
+                if place == BANK_COLS // P - 1:
+                    result = lone_outs.tile([P, BANK_COLS], F32, name="lone_out")
+                    column = t * B + LONE
+                    nc.scalar.activation(
+                        out=result[:], in_=bank[:], func=IDENTITY, bias=bias[:, column : column + 1], scale=1.0
+                    )
+                    rows = slice((q + 1) * BLOCK_ROWS - BANK_COLS // W, (q + 1) * BLOCK_ROWS)
+                    nc.sync.dma_start(
+                        out=out[LONE, t * P : (t + 1) * P, rows, :].rearrange("p r w -> p (r w)"), in_=result[:]
+                    )
+
+            lone_tasks = [None] * 2
+            lone_tasks += [(lone_regroup, (piece,)) for piece in range(4)]
+            lone_tasks += [None, None, None, (lone_quantise, ())]
+            lone_tasks += [(lone_messages, (q,)) for q in range(BLOCKS)]
+            lone_tasks += [(lone_sum, (t, q)) for t in range(D_TILES) for q in range(BLOCKS)]
 
             def fill(b, t, k):
                 bank = banks.tile([P, BANK_COLS], F32, name="bank")
@@ -164,7 +263,7 @@ def tile_graphaugmentation_pa_t_kernel(tc, x, mw, mb, attn_w, out):
                 )
                 return bank[:, 0 : BANK_ROWS * PITCH].rearrange("p (r c) -> p r c", c=PITCH)
 
-            for b in range(B):
+            for b in range(LONE):
                 for pair in range(D_TILES // PAIR):
                     d_tiles = [pair * PAIR + s for s in range(PAIR)]
                     acc = accs.tile([P, PAIR, H * W], F32, name="acc")
@@ -230,9 +329,12 @@ def tile_graphaugmentation_pa_t_kernel(tc, x, mw, mb, attn_w, out):
                             finish(j)
                         before = here
                         step = pair * BANDS + j
-                        if b + 1 < B and step < REGROUP_STEPS:
+                        if b + 1 < LONE and step < REGROUP_STEPS:
                             regroup(nc.scalar.copy, b + 1, step)
-                        if b + 1 < B and step == REGROUP_STEPS:
+                        if b + 1 < LONE and step == REGROUP_STEPS:
                             quantise(b + 1)
+                        turn = (b * (D_TILES // PAIR) + pair) * BANDS + j
+                        if turn < len(lone_tasks) and lone_tasks[turn] is not None:
+                            lone_tasks[turn][0](*lone_tasks[turn][1])
                     vector_adds(0, before, -1)
                     finish(0)

@@ -120,26 +120,30 @@ def tile_graphaugmentation_pa_t_kernel(tc, x, mw, mb, attn_w, out):
 
         ident_rows = ident.rearrange("p (r c) -> p r c", c=W)
         ident_wide = const.tile([P, BLOCK_ROWS, PITCH], F32, name="ident_wide")
-        nc.vector.tensor_copy(out=ident_wide[:, :, PAD : PAD + W], in_=ident_rows)
-        nc.vector.tensor_copy(out=ident_wide[:, :, 0:PAD], in_=ident_rows[:, :, W - PAD : W])
-        nc.vector.tensor_copy(out=ident_wide[:, :, PAD + W : PITCH], in_=ident_rows[:, :, 0:PAD])
         mix = {}
         for step in BLOCK_STEPS:
             mix[step] = const.tile([P, BLOCK_ROWS, W], F32, name="mix%d" % (step + 1))
-            nc.vector.memset(mix[step][:], 0.0)
-        for i, (dy, dx) in enumerate(OFFSETS):
+
+        def build_mix():
+            nc.vector.tensor_copy(out=ident_wide[:, :, PAD : PAD + W], in_=ident_rows)
+            nc.vector.tensor_copy(out=ident_wide[:, :, 0:PAD], in_=ident_rows[:, :, W - PAD : W])
+            nc.vector.tensor_copy(out=ident_wide[:, :, PAD + W : PITCH], in_=ident_rows[:, :, 0:PAD])
             for step in BLOCK_STEPS:
-                shift = dy + BLOCK_ROWS * step
-                low, high = max(0, shift), min(BLOCK_ROWS, BLOCK_ROWS + shift)
-                if low < high:
-                    nc.vector.scalar_tensor_tensor(
-                        out=mix[step][:, low:high, :],
-                        in0=ident_wide[:, low - shift : high - shift, PAD - dx : PAD - dx + W],
-                        scalar=weight[:, i * B + LONE : i * B + LONE + 1],
-                        in1=mix[step][:, low:high, :],
-                        op0=MULT,
-                        op1=ADD,
-                    )
+                nc.vector.memset(mix[step][:], 0.0)
+            for i, (dy, dx) in enumerate(OFFSETS):
+                for step in BLOCK_STEPS:
+                    shift = dy + BLOCK_ROWS * step
+                    low, high = max(0, shift), min(BLOCK_ROWS, BLOCK_ROWS + shift)
+                    if low < high:
+                        nc.vector.scalar_tensor_tensor(
+                            out=mix[step][:, low:high, :],
+                            in0=ident_wide[:, low - shift : high - shift, PAD - dx : PAD - dx + W],
+                            scalar=weight[:, i * B + LONE : i * B + LONE + 1],
+                            in1=mix[step][:, low:high, :],
+                            op0=MULT,
+                            op1=ADD,
+                        )
+
         lone_grouped = const.tile([P, H * W * PACK], BF16, name="lone_grouped", align_bytes=64)
         lone_codes = const.tile([P, H * W], U32, name="lone_codes", align_bytes=64)
         lone_scales = const.tile([P, H * W], U8, name="lone_scales", align_bytes=64)
@@ -181,8 +185,9 @@ def tile_graphaugmentation_pa_t_kernel(tc, x, mw, mb, attn_w, out):
                 out=mw_codes[:].bitcast(FP8X4), scales=mw_scales[:], in_=mw_grouped[:]
             )
             quantise(0)
+        build_mix()
 
-        with tc.psum_pool(name="banks", bufs=6) as banks, tc.psum_pool(name="lone_banks", bufs=2) as lone_banks, tc.tile_pool(
+        with tc.psum_pool(name="banks", bufs=8) as banks, tc.tile_pool(
             name="lone_outs", bufs=2
         ) as lone_outs:
 
@@ -203,7 +208,7 @@ def tile_graphaugmentation_pa_t_kernel(tc, x, mw, mb, attn_w, out):
                 )
 
             def lone_messages(q):
-                bank = lone_banks.tile([P, C], F32, name="lone_bank")
+                bank = banks.tile([P, C], F32, name="bank")
                 cols = slice(q * P, (q + 1) * P)
                 nc.tensor.matmul_mx(
                     out=bank[:],
@@ -221,7 +226,7 @@ def tile_graphaugmentation_pa_t_kernel(tc, x, mw, mb, attn_w, out):
             def lone_sum(t, q):
                 place = q % (BANK_COLS // P)
                 if place == 0:
-                    lone_state["bank"] = lone_banks.tile([P, BANK_COLS], F32, name="lone_bank")
+                    lone_state["bank"] = banks.tile([P, BANK_COLS], F32, name="bank")
                 bank = lone_state["bank"]
                 for step in BLOCK_STEPS:
                     nc.tensor.matmul(

@@ -336,7 +336,7 @@ def tile_graphaugmentation_pa_t_kernel(tc, x, mw, mb, attn_w, out):
                         step = pair * BANDS + j
                         if b + 1 < LONE and step < REGROUP_STEPS:
                             regroup(nc.scalar.copy, b + 1, step)
-                        if b + 1 < LONE and step == REGROUP_STEPS:
+                        if b + 1 < LONE and step == REGROUP_STEPS - 1:
                             quantise(b + 1)
                         turn = (b * (D_TILES // PAIR) + pair) * BANDS + j
                         if turn < len(lone_tasks) and lone_tasks[turn] is not None:

@@ -120,29 +120,27 @@ def tile_graphaugmentation_pa_t_kernel(tc, x, mw, mb, attn_w, out):
 
         ident_rows = ident.rearrange("p (r c) -> p r c", c=W)
         ident_wide = const.tile([P, BLOCK_ROWS, PITCH], F32, name="ident_wide")
+        mix_all = const.tile([P, len(BLOCK_STEPS) * BLOCK_ROWS, W], F32, name="mix_all")
         mix = {}
         for step in BLOCK_STEPS:
-            mix[step] = const.tile([P, BLOCK_ROWS, W], F32, name="mix%d" % (step + 1))
+            mix[step] = mix_all[:, BLOCK_ROWS * (1 - step) : BLOCK_ROWS * (2 - step), :]
 
         def build_mix():
             nc.vector.tensor_copy(out=ident_wide[:, :, PAD : PAD + W], in_=ident_rows)
             nc.vector.tensor_copy(out=ident_wide[:, :, 0:PAD], in_=ident_rows[:, :, W - PAD : W])
             nc.vector.tensor_copy(out=ident_wide[:, :, PAD + W : PITCH], in_=ident_rows[:, :, 0:PAD])
-            for step in BLOCK_STEPS:
-                nc.vector.memset(mix[step][:], 0.0)
-            for i, (dy, dx) in enumerate(OFFSETS):
-                for step in BLOCK_STEPS:
-                    shift = dy + BLOCK_ROWS * step
-                    low, high = max(0, shift), min(BLOCK_ROWS, BLOCK_ROWS + shift)
-                    if low < high:
-                        nc.vector.scalar_tensor_tensor(
-                            out=mix[step][:, low:high, :],
-                            in0=ident_wide[:, low - shift : high - shift, PAD - dx : PAD - dx + W],
-                            scalar=weight[:, i * B + LONE : i * B + LONE + 1],
-                            in1=mix[step][:, low:high, :],
-                            op0=MULT,
-                            op1=ADD,
-                        )
+            nc.vector.memset(mix_all[:], 0.0)
+            for i in (0, 5, 1, 6, 2, 7, 3, 4):
+                dy, dx = OFFSETS[i]
+                rows = slice(dy + BLOCK_ROWS, dy + 2 * BLOCK_ROWS)
+                nc.vector.scalar_tensor_tensor(
+                    out=mix_all[:, rows, :],
+                    in0=ident_wide[:, :, PAD - dx : PAD - dx + W],
+                    scalar=weight[:, i * B + LONE : i * B + LONE + 1],
+                    in1=mix_all[:, rows, :],
+                    op0=MULT,
+                    op1=ADD,
+                )
 
         lone_grouped = const.tile([P, H * W * PACK], BF16, name="lone_grouped", align_bytes=64)
         lone_codes = const.tile([P, H * W], U32, name="lone_codes", align_bytes=64)
@@ -158,10 +156,14 @@ def tile_graphaugmentation_pa_t_kernel(tc, x, mw, mb, attn_w, out):
         with tc.psum_pool(name="prep", bufs=1) as prep:
             mb_t = prep.tile([P, P], F32, name="mb_t")
             nc.tensor.transpose(mb_t[:], mb_rows32[:], ident[:])
-            nc.vector.tensor_copy(out=mb_col[:], in_=mb_t[:, 0:D_TILES])
+            nc.scalar.copy(out=mb_col[:], in_=mb_t[:, 0:D_TILES])
             for t in range(D_TILES):
-                nc.vector.tensor_scalar_mul(
-                    out=bias[:, t * B : (t + 1) * B], in0=weight_sum[:], scalar1=mb_col[:, t : t + 1]
+                nc.scalar.activation(
+                    out=bias[:, t * B : (t + 1) * B],
+                    in_=weight_sum[:],
+                    func=IDENTITY,
+                    bias=0.0,
+                    scale=mb_col[:, t : t + 1],
                 )
 
             for step in range(REGROUP_STEPS):
@@ -177,7 +179,7 @@ def tile_graphaugmentation_pa_t_kernel(tc, x, mw, mb, attn_w, out):
                             mw_words32[:, t * half_c + u : (t + 1) * half_c : 2],
                             ident[:],
                         )
-                nc.vector.tensor_copy(
+                nc.scalar.copy(
                     out=mw_grouped32[:, pair * PAIR : (pair + 1) * PAIR],
                     in_=mw_t.rearrange("p s u d -> p s d u"),
                 )
@@ -334,9 +336,15 @@ def tile_graphaugmentation_pa_t_kernel(tc, x, mw, mb, attn_w, out):
                             finish(j)
                         before = here
                         step = pair * BANDS + j
-                        if b + 1 < LONE and step < REGROUP_STEPS:
-                            regroup(nc.scalar.copy, b + 1, step)
-                        if b + 1 < LONE and step == REGROUP_STEPS - 1:
+                        if b == 0 and step < REGROUP_STEPS:
+                            regroup(nc.scalar.copy, 1, step)
+                        if b == 0 and step == REGROUP_STEPS - 1:
+                            quantise(1)
+                        if b + 2 < LONE and step == 2 * BANDS - 1:
+                            regroup(nc.scalar.copy, b + 2, 0)
+                        if 0 < b and b + 1 < LONE and step < REGROUP_STEPS - 1:
+                            regroup(nc.scalar.copy, b + 1, step + 1)
+                        if 0 < b and b + 1 < LONE and step == REGROUP_STEPS - 2:
                             quantise(b + 1)
                         turn = (b * (D_TILES // PAIR) + pair) * BANDS + j
                         if turn < len(lone_tasks) and lone_tasks[turn] is not None:

@@ -52,6 +52,11 @@ def tile_graphaugmentation_pa_t_kernel(tc, x, mw, mb, attn_w, out):
         name="raws", bufs=LONE
     ) as raws, tc.tile_pool(name="accs", bufs=3) as accs, tc.tile_pool(name="sides", bufs=2) as sides:
         mw_sb = const.tile([P, D_TILES * C], BF16, name="mw_sb")
+        w_bf = const.tile([P, TAPS * B], BF16, name="w_bf")
+        nc.sync.dma_start(out=w_bf[:], in_=attn_w.rearrange("i b -> (i b)").partition_broadcast(P))
+        mb_rows = const.tile([P, P], BF16, name="mb_rows")
+        nc.vector.memset(mb_rows[:], 0.0)
+        nc.sync.dma_start(out=mb_rows[0:D_TILES, :], in_=mb.rearrange("(t p) -> t p", p=P))
         raw_tiles = []
         lone_raw = const.tile([P, PACK, H * W], BF16, name="lone_raw")
         for b in range(LONE):
@@ -59,21 +64,15 @@ def tile_graphaugmentation_pa_t_kernel(tc, x, mw, mb, attn_w, out):
             xb = x[b].rearrange("(p t) h w -> p t (h w)", t=PACK)
             first = (H - ROW0) * W
             nc.sync.dma_start(out=raw[:, :, 0:first], in_=xb[:, :, ROW0 * W : H * W])
-            nc.sync.dma_start(out=raw[:, :, first : ROWS * W], in_=xb[:, :, 0 : ROWS * W - first])
-            raw_tiles.append(raw)
             if b == 0:
                 nc.sync.dma_start(
                     out=mw_sb.rearrange("p (t c) -> p t c", t=D_TILES),
                     in_=mw.rearrange("(t p) c -> p t c", p=P),
                 )
+            nc.sync.dma_start(out=raw[:, :, first : ROWS * W], in_=xb[:, :, 0 : ROWS * W - first])
+            raw_tiles.append(raw)
             if b == 1:
                 nc.sync.dma_start(out=lone_raw[:], in_=x[LONE].rearrange("(p t) h w -> p t (h w)", t=PACK))
-
-        w_bf = const.tile([P, TAPS * B], BF16, name="w_bf")
-        nc.scalar.dma_start(out=w_bf[:], in_=attn_w.rearrange("i b -> (i b)").partition_broadcast(P))
-        mb_rows = const.tile([P, P], BF16, name="mb_rows")
-        nc.vector.memset(mb_rows[:], 0.0)
-        nc.scalar.dma_start(out=mb_rows[0:D_TILES, :], in_=mb.rearrange("(t p) -> t p", p=P))
 
         ident = const.tile([P, P], F32, name="ident")
         make_identity(nc, ident[:])
@@ -93,9 +92,8 @@ def tile_graphaugmentation_pa_t_kernel(tc, x, mw, mb, attn_w, out):
             copy(out=grouped_rows[:, rows, 0:PAD, :], in_=src[:, rows, W - PAD : W, :])
             copy(out=grouped_rows[:, rows, PAD + W : PITCH, :], in_=src[:, rows, 0:PAD, :])
 
-        def quantise(b):
-            start = 0
-            for width in QUANT_WIDTHS:
+        def quantise(b, widths=QUANT_WIDTHS, start=0):
+            for width in widths:
                 words = slice(start // PACK, (start + width) // PACK)
                 nc.vector.quantize_mx(
                     out=x_codes[b % 2][:, words].bitcast(FP8X4),
@@ -166,8 +164,12 @@ def tile_graphaugmentation_pa_t_kernel(tc, x, mw, mb, attn_w, out):
                     scale=mb_col[:, t : t + 1],
                 )
 
-            for step in range(REGROUP_STEPS):
+            build_mix()
+
+            third = WORDS * PACK // 3
+            for step in (0, 1, 2, 3, 4):
                 regroup(nc.scalar.copy if step % 3 == 2 else nc.vector.tensor_copy, 0, step)
+            quantise(0, (third,), 0)
 
             for pair in range(D_TILES // PAIR):
                 mw_t = prep.tile([P, PAIR, 2, P], F32, name="mw_t%d" % pair)
@@ -179,15 +181,15 @@ def tile_graphaugmentation_pa_t_kernel(tc, x, mw, mb, attn_w, out):
                             mw_words32[:, t * half_c + u : (t + 1) * half_c : 2],
                             ident[:],
                         )
-                nc.scalar.copy(
+                (nc.vector.tensor_copy if pair == 0 else nc.scalar.copy)(
                     out=mw_grouped32[:, pair * PAIR : (pair + 1) * PAIR],
                     in_=mw_t.rearrange("p s u d -> p s d u"),
                 )
+            regroup(nc.scalar.copy, 0, 5)
             nc.vector.quantize_mx(
                 out=mw_codes[:].bitcast(FP8X4), scales=mw_scales[:], in_=mw_grouped[:]
             )
-            quantise(0)
-        build_mix()
+            quantise(0, (third, third), third)
 
         with tc.psum_pool(name="banks", bufs=8) as banks, tc.tile_pool(
             name="lone_outs", bufs=2
@@ -292,6 +294,9 @@ def tile_graphaugmentation_pa_t_kernel(tc, x, mw, mb, attn_w, out):
                                     bias=bias[:, column : column + 1] if i == 0 else 0.0,
                                     scale=weight[:, i * B + b : i * B + b + 1],
                                 )
+                        nc.gpsimd.tensor_tensor(
+                            out=side_a[:, :, pixels], in0=side_a[:, :, pixels], in1=side_b[:, :, pixels], op=ADD
+                        )
 
                     def vector_adds(j, source, source_step):
                         pixels = slice(j * BAND * W, (j + 1) * BAND * W)
@@ -312,9 +317,6 @@ def tile_graphaugmentation_pa_t_kernel(tc, x, mw, mb, attn_w, out):
 
                     def finish(j):
                         pixels = slice(j * BAND * W, (j + 1) * BAND * W)
-                        nc.gpsimd.tensor_tensor(
-                            out=side_a[:, :, pixels], in0=side_a[:, :, pixels], in1=side_b[:, :, pixels], op=ADD
-                        )
                         nc.gpsimd.tensor_tensor(
                             out=acc[:, :, pixels], in0=acc[:, :, pixels], in1=side_a[:, :, pixels], op=ADD
                         )

@@ -254,6 +254,7 @@ def tile_graphaugmentation_pa_t_kernel(tc, x, mw, mb, attn_w, out):
             lone_tasks = [None] * 2
             lone_tasks += [(lone_regroup, (piece,)) for piece in range(4)]
             lone_tasks += [None, None, None, (lone_quantise, ())]
+            lone_tasks += [None, None]
             lone_tasks += [(lone_messages, (q,)) for q in range(BLOCKS)]
             lone_tasks += [(lone_sum, (t, q)) for t in range(D_TILES) for q in range(BLOCKS)]
 
@@ -317,7 +318,8 @@ def tile_graphaugmentation_pa_t_kernel(tc, x, mw, mb, attn_w, out):
 
                     def finish(j):
                         pixels = slice(j * BAND * W, (j + 1) * BAND * W)
-                        nc.gpsimd.tensor_tensor(
+                        last = b == LONE - 1 and pair == D_TILES // PAIR - 1 and j == 0
+                        (nc.vector if last else nc.gpsimd).tensor_tensor(
                             out=acc[:, :, pixels], in0=acc[:, :, pixels], in1=side_a[:, :, pixels], op=ADD
                         )
                         nc.sync.dma_start(

@@ -79,18 +79,20 @@ def tile_graphaugmentation_pa_t_kernel(tc, x, mw, mb, attn_w, out):
 
         grouped = const.tile([P, WORDS * PACK], BF16, name="grouped", align_bytes=64)
         nc.vector.memset(grouped[:, ROWS * PITCH * PACK :], 0.0)
-        grouped_rows = grouped[:, 0 : ROWS * PITCH * PACK].rearrange(
-            "p (r c t) -> p r c t", c=PITCH, t=PACK
+        grouped_blocks = grouped[:, 0 : ROWS * PITCH * PACK].rearrange(
+            "p (r c i t) -> p r c t i", c=PITCH // PAD, i=PAD, t=PACK
         )
         x_codes = [const.tile([P, WORDS], U32, name="x_codes%d" % s, align_bytes=64) for s in range(2)]
         x_scales = [const.tile([P, WORDS], U8, name="x_scales%d" % s, align_bytes=64) for s in range(2)]
 
         def regroup(copy, b, step):
             rows = slice(step * REGROUP_ROWS, (step + 1) * REGROUP_ROWS)
-            src = raw_tiles[b].rearrange("p t (r w) -> p r w t", w=W)
-            copy(out=grouped_rows[:, rows, PAD : PAD + W, :], in_=src[:, rows, :, :])
-            copy(out=grouped_rows[:, rows, 0:PAD, :], in_=src[:, rows, W - PAD : W, :])
-            copy(out=grouped_rows[:, rows, PAD + W : PITCH, :], in_=src[:, rows, 0:PAD, :])
+            src = raw_tiles[b].rearrange("p t (r c i) -> p r c t i", c=W // PAD, i=PAD)
+            dst = grouped_blocks
+            last = W // PAD - 1
+            copy(out=dst[:, rows, 1 : 1 + W // PAD], in_=src[:, rows])
+            copy(out=dst[:, rows, 0], in_=src[:, rows, last])
+            copy(out=dst[:, rows, 1 + W // PAD], in_=src[:, rows, 0])
 
         def quantise(b, widths=QUANT_WIDTHS, start=0):
             for width in widths:
@@ -196,10 +198,10 @@ def tile_graphaugmentation_pa_t_kernel(tc, x, mw, mb, attn_w, out):
         ) as lone_outs:
 
             def lone_regroup(piece):
-                pixels = slice(piece * H * W // 4, (piece + 1) * H * W // 4)
+                groups = slice(piece * H * W // PAD // 4, (piece + 1) * H * W // PAD // 4)
                 nc.gpsimd.tensor_scalar(
-                    out=lone_grouped.rearrange("p (n t) -> p n t", t=PACK)[:, pixels, :],
-                    in0=lone_raw.rearrange("p t n -> p n t")[:, pixels, :],
+                    out=lone_grouped.rearrange("p (n i t) -> p n t i", t=PACK, i=PAD)[:, groups],
+                    in0=lone_raw.rearrange("p t (n i) -> p n t i", i=PAD)[:, groups],
                     scalar1=1.0,
                     scalar2=0.0,
                     op0=MULT,

@@ -19,7 +19,9 @@ P = 128
 PACK = 4
 D_TILES = C // P
 PAIR = 2
+PAIRS = D_TILES // PAIR
 
+LOOPED = 5
 PAD = 4
 PITCH = W + 2 * PAD
 ROW0 = 2
@@ -34,10 +36,15 @@ REGROUP_ROWS = 6
 REGROUP_STEPS = ROWS // REGROUP_ROWS
 SCALAR_TAPS = 3
 
-LONE = B - 1
-BLOCK_ROWS = P // W
-BLOCKS = H // BLOCK_ROWS
-BLOCK_STEPS = (-1, 0, 1)
+MATRIX = B - LOOPED
+GROUPS = 8
+GROUP_ROWS = H // GROUPS
+MIXED = [i for i in range(TAPS) if abs(OFFSETS[i][0]) == GROUPS // 2]
+MOVED = [i for i in range(TAPS) if i not in MIXED]
+LOTS = MATRIX * PAIRS
+LOT_TURNS = 5
+FIRST_LOT = 3
+PRODUCT_ENGINES = ("gpsimd", "scalar", "gpsimd", "vector")
 
 
 def tap_window(dy, dx):
@@ -49,30 +56,45 @@ def tap_window(dy, dx):
 def tile_graphaugmentation_pa_t_kernel(tc, x, mw, mb, attn_w, out):
     nc = tc.nc
     with tc.manual_schedule(), tc.tile_pool(name="const", bufs=1) as const, tc.tile_pool(
-        name="raws", bufs=LONE
-    ) as raws, tc.tile_pool(name="accs", bufs=3) as accs, tc.tile_pool(name="sides", bufs=2) as sides:
+        name="raws", bufs=4
+    ) as raws, tc.tile_pool(name="m_raws", bufs=2) as m_raws, tc.tile_pool(name="accs", bufs=3) as accs, tc.tile_pool(
+        name="sides", bufs=2
+    ) as sides, tc.tile_pool(name="m_work", bufs=2) as m_work:
         mw_sb = const.tile([P, D_TILES * C], BF16, name="mw_sb")
         w_bf = const.tile([P, TAPS * B], BF16, name="w_bf")
         nc.sync.dma_start(out=w_bf[:], in_=attn_w.rearrange("i b -> (i b)").partition_broadcast(P))
         mb_rows = const.tile([P, P], BF16, name="mb_rows")
         nc.vector.memset(mb_rows[:], 0.0)
         nc.sync.dma_start(out=mb_rows[0:D_TILES, :], in_=mb.rearrange("(t p) -> t p", p=P))
-        raw_tiles = []
-        lone_raw = const.tile([P, PACK, H * W], BF16, name="lone_raw")
-        for b in range(LONE):
+        raw_tiles = {}
+
+        def load_looped(b, between=None):
             raw = raws.tile([P, PACK, ROWS * W], BF16, name="raw")
             xb = x[b].rearrange("(p t) h w -> p t (h w)", t=PACK)
             first = (H - ROW0) * W
             nc.sync.dma_start(out=raw[:, :, 0:first], in_=xb[:, :, ROW0 * W : H * W])
-            if b == 0:
-                nc.sync.dma_start(
-                    out=mw_sb.rearrange("p (t c) -> p t c", t=D_TILES),
-                    in_=mw.rearrange("(t p) c -> p t c", p=P),
-                )
+            if between is not None:
+                between()
             nc.sync.dma_start(out=raw[:, :, first : ROWS * W], in_=xb[:, :, 0 : ROWS * W - first])
-            raw_tiles.append(raw)
-            if b == 1:
-                nc.sync.dma_start(out=lone_raw[:], in_=x[LONE].rearrange("(p t) h w -> p t (h w)", t=PACK))
+            raw_tiles[b] = raw
+
+        def load_matrix(a):
+            raw = m_raws.tile([P, PACK, H * W], BF16, name="m_raw")
+            nc.sync.dma_start(out=raw[:], in_=x[LOOPED + a].rearrange("(p t) h w -> p t (h w)", t=PACK))
+            raw_tiles[LOOPED + a] = raw
+
+        def load_mw():
+            nc.sync.dma_start(
+                out=mw_sb.rearrange("p (t c) -> p t c", t=D_TILES),
+                in_=mw.rearrange("(t p) c -> p t c", p=P),
+            )
+
+        load_looped(0, load_mw)
+        load_matrix(0)
+        load_looped(1)
+        load_looped(2)
+        load_matrix(1)
+        load_looped(3)
 
         ident = const.tile([P, P], F32, name="ident")
         make_identity(nc, ident[:])
@@ -88,11 +110,10 @@ def tile_graphaugmentation_pa_t_kernel(tc, x, mw, mb, attn_w, out):
         def regroup(copy, b, step):
             rows = slice(step * REGROUP_ROWS, (step + 1) * REGROUP_ROWS)
             src = raw_tiles[b].rearrange("p t (r c i) -> p r c t i", c=W // PAD, i=PAD)
-            dst = grouped_blocks
             last = W // PAD - 1
-            copy(out=dst[:, rows, 1 : 1 + W // PAD], in_=src[:, rows])
-            copy(out=dst[:, rows, 0], in_=src[:, rows, last])
-            copy(out=dst[:, rows, 1 + W // PAD], in_=src[:, rows, 0])
+            copy(out=grouped_blocks[:, rows, 1 : 1 + W // PAD], in_=src[:, rows])
+            copy(out=grouped_blocks[:, rows, 0], in_=src[:, rows, last])
+            copy(out=grouped_blocks[:, rows, 1 + W // PAD], in_=src[:, rows, 0])
 
         def quantise(b, widths=QUANT_WIDTHS, start=0):
             for width in widths:
@@ -106,6 +127,10 @@ def tile_graphaugmentation_pa_t_kernel(tc, x, mw, mb, attn_w, out):
 
         weight = const.tile([P, TAPS * B], F32, name="weight")
         nc.vector.tensor_copy(out=weight[:], in_=w_bf[:])
+
+        def weight_of(i, b):
+            return weight[:, i * B + b : i * B + b + 1]
+
         weight_sum = const.tile([P, B], F32, name="weight_sum")
         nc.vector.tensor_reduce(
             out=weight_sum[:],
@@ -118,34 +143,67 @@ def tile_graphaugmentation_pa_t_kernel(tc, x, mw, mb, attn_w, out):
         mb_col = const.tile([P, D_TILES], F32, name="mb_col")
         bias = const.tile([P, D_TILES * B], F32, name="bias")
 
-        ident_rows = ident.rearrange("p (r c) -> p r c", c=W)
-        ident_wide = const.tile([P, BLOCK_ROWS, PITCH], F32, name="ident_wide")
-        mix_all = const.tile([P, len(BLOCK_STEPS) * BLOCK_ROWS, W], F32, name="mix_all")
-        mix = {}
-        for step in BLOCK_STEPS:
-            mix[step] = mix_all[:, BLOCK_ROWS * (1 - step) : BLOCK_ROWS * (2 - step), :]
+        ident_rows = ident.rearrange("p (k c) -> p k c", c=W)
+        ident_wide = const.tile([P, GROUP_ROWS + 2, PITCH], F32, name="ident_wide")
 
-        def build_mix():
-            nc.vector.tensor_copy(out=ident_wide[:, :, PAD : PAD + W], in_=ident_rows)
-            nc.vector.tensor_copy(out=ident_wide[:, :, 0:PAD], in_=ident_rows[:, :, W - PAD : W])
-            nc.vector.tensor_copy(out=ident_wide[:, :, PAD + W : PITCH], in_=ident_rows[:, :, 0:PAD])
-            nc.vector.memset(mix_all[:], 0.0)
-            for i in (0, 5, 1, 6, 2, 7, 3, 4):
+        def source(dy, r):
+            carry, group = divmod(r - dy, GROUPS)
+            return group, carry
+
+        moves = {}
+        for i in MOVED:
+            for carry in sorted({source(OFFSETS[i][0], r)[1] for r in range(GROUPS)}):
+                moves[i, carry] = const.tile([P, GROUP_ROWS, W], F32, name="move%d_%d" % (i, carry + 1))
+
+        def build_moves():
+            inner = slice(1, 1 + GROUP_ROWS)
+            nc.vector.tensor_copy(out=ident_wide[:, inner, PAD : PAD + W], in_=ident_rows)
+            nc.vector.tensor_copy(out=ident_wide[:, inner, 0:PAD], in_=ident_rows[:, :, W - PAD : W])
+            nc.vector.tensor_copy(out=ident_wide[:, inner, PAD + W : PITCH], in_=ident_rows[:, :, 0:PAD])
+            nc.vector.tensor_copy(out=ident_wide[:, 0, :], in_=ident_wide[:, GROUP_ROWS, :])
+            nc.vector.tensor_copy(out=ident_wide[:, GROUP_ROWS + 1, :], in_=ident_wide[:, 1, :])
+            for (i, carry), move in moves.items():
+                cols = slice(PAD - OFFSETS[i][1], PAD - OFFSETS[i][1] + W)
+                nc.vector.tensor_copy(out=move[:], in_=ident_wide[:, 1 + carry : 1 + carry + GROUP_ROWS, cols])
+
+        mixes = [const.tile([P, GROUP_ROWS + 1, W], F32, name="mix%d" % a) for a in range(MATRIX)]
+
+        def build_mix(a):
+            for i in MIXED:
                 dy, dx = OFFSETS[i]
-                rows = slice(dy + BLOCK_ROWS, dy + 2 * BLOCK_ROWS)
-                nc.vector.scalar_tensor_tensor(
-                    out=mix_all[:, rows, :],
-                    in0=ident_wide[:, :, PAD - dx : PAD - dx + W],
-                    scalar=weight[:, i * B + LONE : i * B + LONE + 1],
-                    in1=mix_all[:, rows, :],
-                    op0=MULT,
-                    op1=ADD,
-                )
+                row = 1 + source(dy, 0)[1]
+                part = ident_wide[:, row : row + GROUP_ROWS + 1, PAD - dx : PAD - dx + W]
+                if i == MIXED[0]:
+                    nc.vector.tensor_scalar_mul(out=mixes[a][:], in0=part, scalar1=weight_of(i, LOOPED + a))
+                else:
+                    nc.vector.scalar_tensor_tensor(
+                        out=mixes[a][:], in0=part, scalar=weight_of(i, LOOPED + a), in1=mixes[a][:], op0=MULT, op1=ADD
+                    )
 
-        lone_grouped = const.tile([P, H * W * PACK], BF16, name="lone_grouped", align_bytes=64)
-        lone_codes = const.tile([P, H * W], U32, name="lone_codes", align_bytes=64)
-        lone_scales = const.tile([P, H * W], U8, name="lone_scales", align_bytes=64)
-        lone_m = const.tile([P, BLOCKS, C], F32, name="lone_m")
+        m_grouped = const.tile([P, H * W * PACK], BF16, name="m_grouped", align_bytes=64)
+        m_codes = [const.tile([P, H * W], U32, name="m_codes%d" % s, align_bytes=64) for s in range(2)]
+        m_scales = [const.tile([P, H * W], U8, name="m_scales%d" % s, align_bytes=64) for s in range(2)]
+
+        def matrix_regroup_gpsimd(a, r):
+            nc.gpsimd.tensor_scalar(
+                out=m_grouped.rearrange("p (r k c t) -> p r k c t", r=GROUPS, c=W, t=PACK)[:, r],
+                in0=raw_tiles[LOOPED + a].rearrange("p t (k r c) -> p r k c t", r=GROUPS, c=W)[:, r],
+                scalar1=1.0,
+                scalar2=0.0,
+                op0=MULT,
+                op1=ADD,
+            )
+
+        def matrix_regroup(a, r):
+            nc.vector.tensor_copy(
+                out=m_grouped.rearrange("p (r k c i t) -> p r k c t i", r=GROUPS, c=W // PAD, i=PAD, t=PACK)[:, r],
+                in_=raw_tiles[LOOPED + a].rearrange("p t (k r c i) -> p r k c t i", r=GROUPS, c=W // PAD, i=PAD)[:, r],
+            )
+
+        def matrix_quantise(a):
+            nc.vector.quantize_mx(
+                out=m_codes[a % 2][:].bitcast(FP8X4), scales=m_scales[a % 2][:], in_=m_grouped[:]
+            )
 
         mw_words32 = mw_sb[:].bitcast(F32)
         half_c = C // 2
@@ -166,14 +224,15 @@ def tile_graphaugmentation_pa_t_kernel(tc, x, mw, mb, attn_w, out):
                     scale=mb_col[:, t : t + 1],
                 )
 
-            build_mix()
+            build_moves()
+            build_mix(0)
 
             third = WORDS * PACK // 3
             for step in (0, 1, 2, 3, 4):
                 regroup(nc.scalar.copy if step % 3 == 2 else nc.vector.tensor_copy, 0, step)
             quantise(0, (third,), 0)
 
-            for pair in range(D_TILES // PAIR):
+            for pair in range(PAIRS):
                 mw_t = prep.tile([P, PAIR, 2, P], F32, name="mw_t%d" % pair)
                 for s in range(PAIR):
                     t = pair * PAIR + s
@@ -193,72 +252,125 @@ def tile_graphaugmentation_pa_t_kernel(tc, x, mw, mb, attn_w, out):
             )
             quantise(0, (third, third), third)
 
-        with tc.psum_pool(name="banks", bufs=8) as banks, tc.tile_pool(
-            name="lone_outs", bufs=2
-        ) as lone_outs:
+            for r in range(GROUPS):
+                matrix_regroup_gpsimd(0, r)
 
-            def lone_regroup(piece):
-                groups = slice(piece * H * W // PAD // 4, (piece + 1) * H * W // PAD // 4)
-                nc.gpsimd.tensor_scalar(
-                    out=lone_grouped.rearrange("p (n i t) -> p n t i", t=PACK, i=PAD)[:, groups],
-                    in0=lone_raw.rearrange("p t (n i) -> p n t i", i=PAD)[:, groups],
-                    scalar1=1.0,
-                    scalar2=0.0,
-                    op0=MULT,
-                    op1=ADD,
-                )
+        load_looped(4)
+        load_matrix(2)
 
-            def lone_quantise():
-                nc.vector.quantize_mx(
-                    out=lone_codes[:].bitcast(FP8X4), scales=lone_scales[:], in_=lone_grouped[:]
-                )
+        with tc.psum_pool(name="banks", bufs=6) as banks, tc.psum_pool(name="m_banks", bufs=2) as m_banks:
 
-            def lone_messages(q):
-                bank = banks.tile([P, C], F32, name="bank")
-                cols = slice(q * P, (q + 1) * P)
-                nc.tensor.matmul_mx(
-                    out=bank[:],
-                    lhsT=lone_codes[:, cols].bitcast(FP8X4),
-                    lhsT_scale=lone_scales[:, cols],
-                    rhs=mw_codes[:].bitcast(FP8X4),
-                    rhs_scale=mw_scales[:],
-                    start=True,
-                    stop=True,
-                )
-                nc.scalar.copy(out=lone_m[:, q, :], in_=bank[:])
+            m_tiles = {}
+            m_products = {}
 
-            lone_state = {}
+            def matrix_messages(lot, u):
+                a, pair = divmod(lot, PAIRS)
+                if u == 0:
+                    m_tiles[lot] = m_work.tile([P, GROUPS, PAIR * P], F32, name="m_tile")
+                bank = m_banks.tile([P, 2, PAIR * P], F32, name="m_bank")
+                d_cols = slice(pair * PAIR * P, (pair + 1) * PAIR * P)
+                for v in range(2):
+                    cols = slice((2 * u + v) * P, (2 * u + v + 1) * P)
+                    nc.tensor.matmul_mx(
+                        out=bank[:, v, :],
+                        lhsT=m_codes[a % 2][:, cols].bitcast(FP8X4),
+                        lhsT_scale=m_scales[a % 2][:, cols],
+                        rhs=mw_codes[:, d_cols].bitcast(FP8X4),
+                        rhs_scale=mw_scales[:, d_cols],
+                        start=True,
+                        stop=True,
+                    )
+                nc.scalar.copy(out=m_tiles[lot][:, 2 * u : 2 * u + 2, :], in_=bank[:])
 
-            def lone_sum(t, q):
-                place = q % (BANK_COLS // P)
-                if place == 0:
-                    lone_state["bank"] = banks.tile([P, BANK_COLS], F32, name="bank")
-                bank = lone_state["bank"]
-                for step in BLOCK_STEPS:
+            def matrix_product(lot, s, e):
+                product = m_work.tile([P, GROUPS, P], F32, name="m_product%d" % e)
+                m_products[lot, s, e] = product
+                m = m_tiles[lot][:, :, s * P : (s + 1) * P]
+                scale = weight_of(MOVED[e], LOOPED + lot // PAIRS)
+                engine = PRODUCT_ENGINES[e]
+                if engine == "gpsimd":
+                    nc.gpsimd.tensor_scalar(out=product[:], in0=m, scalar1=scale, scalar2=0.0, op0=MULT, op1=ADD)
+                elif engine == "scalar":
+                    nc.scalar.activation(out=product[:], in_=m, func=IDENTITY, bias=0.0, scale=scale)
+                else:
+                    nc.vector.tensor_scalar_mul(out=product[:], in0=m, scalar1=scale)
+
+            def matrix_sum(lot, s, half):
+                bank = m_banks.tile([P, 2, PAIR * P], F32, name="m_bank").rearrange("p v d -> p (v d)")
+                for place in range(GROUPS // 2):
+                    r = half * GROUPS // 2 + place
+                    pixels = bank[:, place * P : (place + 1) * P]
+                    group, carry = source(-(GROUPS // 2), r)
                     nc.tensor.matmul(
-                        out=bank[:, place * P : (place + 1) * P],
-                        lhsT=lone_m[:, (q + step) % BLOCKS, t * P : (t + 1) * P],
-                        rhs=mix[step].rearrange("p r c -> p (r c)"),
-                        start=step == BLOCK_STEPS[0],
-                        stop=step == BLOCK_STEPS[-1],
+                        out=pixels,
+                        lhsT=m_tiles[lot][:, group, s * P : (s + 1) * P],
+                        rhs=mixes[lot // PAIRS][:, carry : carry + GROUP_ROWS, :].rearrange("p k c -> p (k c)"),
+                        start=True,
+                        stop=False,
                     )
-                if place == BANK_COLS // P - 1:
-                    result = lone_outs.tile([P, BANK_COLS], F32, name="lone_out")
-                    column = t * B + LONE
-                    nc.scalar.activation(
-                        out=result[:], in_=bank[:], func=IDENTITY, bias=bias[:, column : column + 1], scale=1.0
-                    )
-                    rows = slice((q + 1) * BLOCK_ROWS - BANK_COLS // W, (q + 1) * BLOCK_ROWS)
+                    for e, i in enumerate(MOVED):
+                        group, carry = source(OFFSETS[i][0], r)
+                        nc.tensor.matmul(
+                            out=pixels,
+                            lhsT=m_products[lot, s, e][:, group, :],
+                            rhs=moves[i, carry].rearrange("p k c -> p (k c)"),
+                            is_transpose=True,
+                            start=False,
+                            stop=e == len(MOVED) - 1,
+                        )
+                return bank
+
+            m_outs = {}
+
+            def matrix_leave(lot, s, half, bank):
+                a, pair = divmod(lot, PAIRS)
+                t = pair * PAIR + s
+                if half == 0:
+                    m_outs[lot, s] = m_work.tile([P, H * W], F32, name="m_out")
+                result = m_outs[lot, s]
+                column = t * B + LOOPED + a
+                rows = slice(half * GROUPS // 2, (half + 1) * GROUPS // 2)
+                nc.scalar.activation(
+                    out=result.rearrange("p (k r c) -> p r k c", r=GROUPS, c=W)[:, rows],
+                    in_=bank.rearrange("p (r k c) -> p r k c", k=GROUP_ROWS, c=W),
+                    func=IDENTITY,
+                    bias=bias[:, column : column + 1],
+                    scale=1.0,
+                )
+                if half == 1:
                     nc.sync.dma_start(
-                        out=out[LONE, t * P : (t + 1) * P, rows, :].rearrange("p r w -> p (r w)"), in_=result[:]
+                        out=out[LOOPED + a, t * P : (t + 1) * P].rearrange("p r w -> p (r w)"), in_=result[:]
                     )
 
-            lone_tasks = [None] * 2
-            lone_tasks += [(lone_regroup, (piece,)) for piece in range(4)]
-            lone_tasks += [None, None, None, (lone_quantise, ())]
-            lone_tasks += [None, None]
-            lone_tasks += [(lone_messages, (q,)) for q in range(BLOCKS)]
-            lone_tasks += [(lone_sum, (t, q)) for t in range(D_TILES) for q in range(BLOCKS)]
+            turns = (LOOPED * PAIRS) * BANDS
+            tasks = [[] for turn in range(turns + 1)]
+            for q in range(LOTS):
+                base = FIRST_LOT + LOT_TURNS * q
+                if q % PAIRS == 0:
+                    a = q // PAIRS
+                    if a > 0:
+                        for r in range(GROUPS):
+                            tasks[base - 5 + r // 4].append((matrix_regroup, (a, r)))
+                    tasks[max(base - 3, 1)].append((matrix_quantise, (a,)))
+                    if a > 0:
+                        tasks[base - 6].append((build_mix, (a,)))
+            leaving = []
+
+            def start_sum(lot, s, half):
+                leaving.append((lot, s, half, matrix_sum(lot, s, half)))
+
+            for q in range(LOTS):
+                base = FIRST_LOT + LOT_TURNS * q
+                for u in range(GROUPS // 2):
+                    tasks[base].append((matrix_messages, (q, u)))
+                for s in range(PAIR):
+                    for half in range(2):
+                        tasks[base + 6 + 2 * s + half].append((start_sum, (q, s, half)))
+            for q in range(LOTS):
+                base = FIRST_LOT + LOT_TURNS * q
+                for s in range(PAIR):
+                    for e in range(len(MOVED)):
+                        tasks[base + 2 + 2 * s + e // 2].append((matrix_product, (q, s, e)))
 
             def fill(b, t, k):
                 bank = banks.tile([P, BANK_COLS], F32, name="bank")
@@ -275,8 +387,8 @@ def tile_graphaugmentation_pa_t_kernel(tc, x, mw, mb, attn_w, out):
                 )
                 return bank[:, 0 : BANK_ROWS * PITCH].rearrange("p (r c) -> p r c", c=PITCH)
 
-            for b in range(LONE):
-                for pair in range(D_TILES // PAIR):
+            for b in range(LOOPED):
+                for pair in range(PAIRS):
                     d_tiles = [pair * PAIR + s for s in range(PAIR)]
                     acc = accs.tile([P, PAIR, H * W], F32, name="acc")
                     side_a = sides.tile([P, PAIR, H * W], F32, name="side_a")
@@ -295,13 +407,13 @@ def tile_graphaugmentation_pa_t_kernel(tc, x, mw, mb, attn_w, out):
                                     in_=banks_j[s][:, row : row + BAND, col : col + W],
                                     func=IDENTITY,
                                     bias=bias[:, column : column + 1] if i == 0 else 0.0,
-                                    scale=weight[:, i * B + b : i * B + b + 1],
+                                    scale=weight_of(i, b),
                                 )
                         nc.gpsimd.tensor_tensor(
                             out=side_a[:, :, pixels], in0=side_a[:, :, pixels], in1=side_b[:, :, pixels], op=ADD
                         )
 
-                    def vector_adds(j, source, source_step):
+                    def vector_adds(j, source_banks, source_step):
                         pixels = slice(j * BAND * W, (j + 1) * BAND * W)
                         for i in range(SCALAR_TAPS, TAPS):
                             bank_step, row, col = tap_window(*OFFSETS[i])
@@ -311,8 +423,8 @@ def tile_graphaugmentation_pa_t_kernel(tc, x, mw, mb, attn_w, out):
                                 band = acc[:, s, pixels].rearrange("p (r c) -> p r c", c=W)
                                 nc.vector.scalar_tensor_tensor(
                                     out=band,
-                                    in0=source[s][:, row : row + BAND, col : col + W],
-                                    scalar=weight[:, i * B + b : i * B + b + 1],
+                                    in0=source_banks[s][:, row : row + BAND, col : col + W],
+                                    scalar=weight_of(i, b),
                                     in1=band,
                                     op0=MULT,
                                     op1=ADD,
@@ -320,7 +432,7 @@ def tile_graphaugmentation_pa_t_kernel(tc, x, mw, mb, attn_w, out):
 
                     def finish(j):
                         pixels = slice(j * BAND * W, (j + 1) * BAND * W)
-                        last = b == LONE - 1 and pair == D_TILES // PAIR - 1 and j == 0
+                        last = b == LOOPED - 1 and pair == PAIRS - 1 and j == 0
                         (nc.vector if last else nc.gpsimd).tensor_tensor(
                             out=acc[:, :, pixels], in0=acc[:, :, pixels], in1=side_a[:, :, pixels], op=ADD
                         )
@@ -335,6 +447,12 @@ def tile_graphaugmentation_pa_t_kernel(tc, x, mw, mb, attn_w, out):
                     for j in range(BANDS):
                         here = [fill(b, t, j) for t in d_tiles]
                         scalar_products(j, here)
+                        for parts in leaving:
+                            matrix_leave(*parts)
+                        leaving.clear()
+                        turn = (b * PAIRS + pair) * BANDS + j
+                        for task, arguments in tasks[turn]:
+                            task(*arguments)
                         if j > 0:
                             vector_adds(j, before, -1)
                         vector_adds(j, here, 0)
@@ -346,14 +464,13 @@ def tile_graphaugmentation_pa_t_kernel(tc, x, mw, mb, attn_w, out):
                             regroup(nc.scalar.copy, 1, step)
                         if b == 0 and step == REGROUP_STEPS - 1:
                             quantise(1)
-                        if b + 2 < LONE and step == 2 * BANDS - 1:
+                        if b + 2 < LOOPED and step == 2 * BANDS - 1:
                             regroup(nc.scalar.copy, b + 2, 0)
-                        if 0 < b and b + 1 < LONE and step < REGROUP_STEPS - 1:
+                        if 0 < b and b + 1 < LOOPED and step < REGROUP_STEPS - 1:
                             regroup(nc.scalar.copy, b + 1, step + 1)
-                        if 0 < b and b + 1 < LONE and step == REGROUP_STEPS - 2:
+                        if 0 < b and b + 1 < LOOPED and step == REGROUP_STEPS - 2:
                             quantise(b + 1)
-                        turn = (b * (D_TILES // PAIR) + pair) * BANDS + j
-                        if turn < len(lone_tasks) and lone_tasks[turn] is not None:
-                            lone_tasks[turn][0](*lone_tasks[turn][1])
                     vector_adds(0, before, -1)
                     finish(0)
+            for parts in leaving:
+                matrix_leave(*parts)

@@ -42,9 +42,9 @@ GROUP_ROWS = H // GROUPS
 MIXED = [i for i in range(TAPS) if abs(OFFSETS[i][0]) == GROUPS // 2]
 MOVED = [i for i in range(TAPS) if i not in MIXED]
 LOTS = MATRIX * PAIRS
-LOT_TURNS = 5
-FIRST_LOT = 3
-PRODUCT_ENGINES = ("gpsimd", "scalar", "gpsimd", "vector")
+BLOCKS_A_TURN = 3
+FIRST_BLOCK = 6
+PRODUCT_ENGINES = ("gpsimd", "gpsimd", "gpsimd", "vector")
 
 
 def tap_window(dy, dx):
@@ -262,12 +262,20 @@ def tile_graphaugmentation_pa_t_kernel(tc, x, mw, mb, attn_w, out):
 
             m_tiles = {}
             m_products = {}
+            m_holders = []
+            leaving = []
+
+            def m_bank(holder):
+                m_holders.append(holder)
+                if len(m_holders) > 2 and m_holders[-3] in leaving:
+                    matrix_leave()
+                return m_banks.tile([P, 2, PAIR * P], F32, name="m_bank")
 
             def matrix_messages(lot, u):
                 a, pair = divmod(lot, PAIRS)
                 if u == 0:
                     m_tiles[lot] = m_work.tile([P, GROUPS, PAIR * P], F32, name="m_tile")
-                bank = m_banks.tile([P, 2, PAIR * P], F32, name="m_bank")
+                bank = m_bank(None)
                 d_cols = slice(pair * PAIR * P, (pair + 1) * PAIR * P)
                 for v in range(2):
                     cols = slice((2 * u + v) * P, (2 * u + v + 1) * P)
@@ -295,34 +303,46 @@ def tile_graphaugmentation_pa_t_kernel(tc, x, mw, mb, attn_w, out):
                 else:
                     nc.vector.tensor_scalar_mul(out=product[:], in0=m, scalar1=scale)
 
-            def matrix_sum(lot, s, half):
-                bank = m_banks.tile([P, 2, PAIR * P], F32, name="m_bank").rearrange("p v d -> p (v d)")
-                for place in range(GROUPS // 2):
-                    r = half * GROUPS // 2 + place
-                    pixels = bank[:, place * P : (place + 1) * P]
+            m_sums = {}
+
+            def matrix_block(lot, s, r):
+                half, place = divmod(r, GROUPS // 2)
+                if place == 0:
+                    m_sums[lot, s, half] = m_bank((lot, s, half)).rearrange("p v d -> p (v d)")
+                pixels = m_sums[lot, s, half][:, place * P : (place + 1) * P]
+
+                def mixed(start):
                     group, carry = source(-(GROUPS // 2), r)
                     nc.tensor.matmul(
                         out=pixels,
                         lhsT=m_tiles[lot][:, group, s * P : (s + 1) * P],
                         rhs=mixes[lot // PAIRS][:, carry : carry + GROUP_ROWS, :].rearrange("p k c -> p (k c)"),
-                        start=True,
-                        stop=False,
+                        start=start,
+                        stop=not start,
                     )
-                    for e, i in enumerate(MOVED):
-                        group, carry = source(OFFSETS[i][0], r)
-                        nc.tensor.matmul(
-                            out=pixels,
-                            lhsT=m_products[lot, s, e][:, group, :],
-                            rhs=moves[i, carry].rearrange("p k c -> p (k c)"),
-                            is_transpose=True,
-                            start=False,
-                            stop=e == len(MOVED) - 1,
-                        )
-                return bank
+
+                if r % 2 == 0:
+                    mixed(True)
+                for e, i in enumerate(MOVED):
+                    group, carry = source(OFFSETS[i][0], r)
+                    nc.tensor.matmul(
+                        out=pixels,
+                        lhsT=m_products[lot, s, e][:, group, :],
+                        rhs=moves[i, carry].rearrange("p k c -> p (k c)"),
+                        is_transpose=True,
+                        start=e == 0 and r % 2 == 1,
+                        stop=e == len(MOVED) - 1 and r % 2 == 0,
+                    )
+                if r % 2 == 1:
+                    mixed(False)
+                if place == GROUPS // 2 - 1:
+                    leaving.append((lot, s, half))
 
             m_outs = {}
 
-            def matrix_leave(lot, s, half, bank):
+            def matrix_leave():
+                lot, s, half = leaving.pop(0)
+                bank = m_sums[lot, s, half]
                 a, pair = divmod(lot, PAIRS)
                 t = pair * PAIR + s
                 if half == 0:
@@ -342,35 +362,35 @@ def tile_graphaugmentation_pa_t_kernel(tc, x, mw, mb, attn_w, out):
                         out=out[LOOPED + a, t * P : (t + 1) * P].rearrange("p r w -> p (r w)"), in_=result[:]
                     )
 
-            turns = (LOOPED * PAIRS) * BANDS
-            tasks = [[] for turn in range(turns + 1)]
-            for q in range(LOTS):
-                base = FIRST_LOT + LOT_TURNS * q
-                if q % PAIRS == 0:
-                    a = q // PAIRS
-                    if a > 0:
-                        for r in range(GROUPS):
-                            tasks[base - 5 + r // 4].append((matrix_regroup, (a, r)))
-                    tasks[max(base - 3, 1)].append((matrix_quantise, (a,)))
-                    if a > 0:
-                        tasks[base - 6].append((build_mix, (a,)))
-            leaving = []
-
-            def start_sum(lot, s, half):
-                leaving.append((lot, s, half, matrix_sum(lot, s, half)))
-
-            for q in range(LOTS):
-                base = FIRST_LOT + LOT_TURNS * q
-                for u in range(GROUPS // 2):
-                    tasks[base].append((matrix_messages, (q, u)))
-                for s in range(PAIR):
-                    for half in range(2):
-                        tasks[base + 6 + 2 * s + half].append((start_sum, (q, s, half)))
-            for q in range(LOTS):
-                base = FIRST_LOT + LOT_TURNS * q
-                for s in range(PAIR):
-                    for e in range(len(MOVED)):
-                        tasks[base + 2 + 2 * s + e // 2].append((matrix_product, (q, s, e)))
+            def matrix_turn(turn):
+                messages = []
+                for q in range(LOTS):
+                    base = FIRST_BLOCK + 2 * GROUPS * q // BLOCKS_A_TURN
+                    a, pair = divmod(q, PAIRS)
+                    if pair == 0:
+                        if a > 0 and base - 9 <= turn < base - 7:
+                            for r in range(GROUPS // 2):
+                                matrix_regroup(a, r + (turn - base + 9) * GROUPS // 2)
+                        if turn == base - 10 and a > 0:
+                            build_mix(a)
+                        if turn == max(base - 7, 1):
+                            matrix_quantise(a)
+                    if turn == base - 4:
+                        messages = [(q, u) for u in range(GROUPS // 2)]
+                first = (turn - FIRST_BLOCK) * BLOCKS_A_TURN
+                for block in range(first, first + BLOCKS_A_TURN + 1):
+                    if block % (GROUPS // 2) == 0:
+                        for q, u in messages:
+                            matrix_messages(q, u)
+                        messages = []
+                    if block < first + BLOCKS_A_TURN and 0 <= block < LOTS * PAIR * GROUPS:
+                        matrix_block(block // (PAIR * GROUPS), block // GROUPS % PAIR, block % GROUPS)
+                for q in range(LOTS):
+                    for s in range(PAIR):
+                        base = FIRST_BLOCK + (2 * q + s) * GROUPS // BLOCKS_A_TURN
+                        for e in range(len(MOVED)):
+                            if turn == base - 3 + e // 2:
+                                matrix_product(q, s, e)
 
             def fill(b, t, k):
                 bank = banks.tile([P, BANK_COLS], F32, name="bank")
@@ -387,6 +407,12 @@ def tile_graphaugmentation_pa_t_kernel(tc, x, mw, mb, attn_w, out):
                 )
                 return bank[:, 0 : BANK_ROWS * PITCH].rearrange("p (r c) -> p r c", c=PITCH)
 
+            def fills(turn):
+                b, rest = divmod(turn, PAIRS * BANDS)
+                pair, j = divmod(rest, BANDS)
+                return [fill(b, pair * PAIR + s, j) for s in range(PAIR)]
+
+            ahead = fills(0)
             for b in range(LOOPED):
                 for pair in range(PAIRS):
                     d_tiles = [pair * PAIR + s for s in range(PAIR)]
@@ -445,16 +471,16 @@ def tile_graphaugmentation_pa_t_kernel(tc, x, mw, mb, attn_w, out):
 
                     before = None
                     for j in range(BANDS):
-                        here = [fill(b, t, j) for t in d_tiles]
+                        here = ahead
                         scalar_products(j, here)
-                        for parts in leaving:
-                            matrix_leave(*parts)
-                        leaving.clear()
-                        turn = (b * PAIRS + pair) * BANDS + j
-                        for task, arguments in tasks[turn]:
-                            task(*arguments)
                         if j > 0:
                             vector_adds(j, before, -1)
+                        while leaving:
+                            matrix_leave()
+                        turn = (b * PAIRS + pair) * BANDS + j
+                        if turn + 1 < LOOPED * PAIRS * BANDS:
+                            ahead = fills(turn + 1)
+                        matrix_turn(turn)
                         vector_adds(j, here, 0)
                         if j > 0:
                             finish(j)
@@ -472,5 +498,5 @@ def tile_graphaugmentation_pa_t_kernel(tc, x, mw, mb, attn_w, out):
                             quantise(b + 1)
                     vector_adds(0, before, -1)
                     finish(0)
-            for parts in leaving:
-                matrix_leave(*parts)
+            while leaving:
+                matrix_leave()

@@ -44,7 +44,7 @@ MOVED = [i for i in range(TAPS) if i not in MIXED]
 LOTS = MATRIX * PAIRS
 BLOCKS_A_TURN = 3
 FIRST_BLOCK = 6
-PRODUCT_ENGINES = ("gpsimd", "gpsimd", "gpsimd", "vector")
+PRODUCT_ENGINES = (("gpsimd", "vector", "scalar", "gpsimd"), ("gpsimd", "vector", "scalar", "vector"))
 
 
 def tap_window(dy, dx):
@@ -295,7 +295,7 @@ def tile_graphaugmentation_pa_t_kernel(tc, x, mw, mb, attn_w, out):
                 m_products[lot, s, e] = product
                 m = m_tiles[lot][:, :, s * P : (s + 1) * P]
                 scale = weight_of(MOVED[e], LOOPED + lot // PAIRS)
-                engine = PRODUCT_ENGINES[e]
+                engine = PRODUCT_ENGINES[s][e]
                 if engine == "gpsimd":
                     nc.gpsimd.tensor_scalar(out=product[:], in0=m, scalar1=scale, scalar2=0.0, op0=MULT, op1=ADD)
                 elif engine == "scalar":

@@ -34,7 +34,7 @@ WORDS = 1536
 QUANT_WIDTHS = (4096, 2048)
 REGROUP_ROWS = 6
 REGROUP_STEPS = ROWS // REGROUP_ROWS
-SCALAR_TAPS = 3
+SCALAR_TAPS = 2
 
 MATRIX = B - LOOPED
 GROUPS = 8
@@ -44,7 +44,7 @@ MOVED = [i for i in range(TAPS) if i not in MIXED]
 LOTS = MATRIX * PAIRS
 BLOCKS_A_TURN = 3
 FIRST_BLOCK = 6
-PRODUCT_ENGINES = (("gpsimd", "vector", "scalar", "gpsimd"), ("gpsimd", "vector", "scalar", "vector"))
+PRODUCT_ENGINES = ("gpsimd", "gpsimd", "gpsimd", "scalar")
 
 
 def tap_window(dy, dx):
@@ -195,7 +195,7 @@ def tile_graphaugmentation_pa_t_kernel(tc, x, mw, mb, attn_w, out):
             )
 
         def matrix_regroup(a, r):
-            nc.vector.tensor_copy(
+            nc.scalar.copy(
                 out=m_grouped.rearrange("p (r k c i t) -> p r k c t i", r=GROUPS, c=W // PAD, i=PAD, t=PACK)[:, r],
                 in_=raw_tiles[LOOPED + a].rearrange("p t (k r c i) -> p r k c t i", r=GROUPS, c=W // PAD, i=PAD)[:, r],
             )
@@ -295,13 +295,11 @@ def tile_graphaugmentation_pa_t_kernel(tc, x, mw, mb, attn_w, out):
                 m_products[lot, s, e] = product
                 m = m_tiles[lot][:, :, s * P : (s + 1) * P]
                 scale = weight_of(MOVED[e], LOOPED + lot // PAIRS)
-                engine = PRODUCT_ENGINES[s][e]
+                engine = PRODUCT_ENGINES[e]
                 if engine == "gpsimd":
                     nc.gpsimd.tensor_scalar(out=product[:], in0=m, scalar1=scale, scalar2=0.0, op0=MULT, op1=ADD)
-                elif engine == "scalar":
-                    nc.scalar.activation(out=product[:], in_=m, func=IDENTITY, bias=0.0, scale=scale)
                 else:
-                    nc.vector.tensor_scalar_mul(out=product[:], in0=m, scalar1=scale)
+                    nc.scalar.activation(out=product[:], in_=m, func=IDENTITY, bias=0.0, scale=scale)
 
             m_sums = {}
 
@@ -418,8 +416,7 @@ def tile_graphaugmentation_pa_t_kernel(tc, x, mw, mb, attn_w, out):
                     d_tiles = [pair * PAIR + s for s in range(PAIR)]
                     acc = accs.tile([P, PAIR, H * W], F32, name="acc")
                     side_a = sides.tile([P, PAIR, H * W], F32, name="side_a")
-                    side_b = sides.tile([P, PAIR, H * W], F32, name="side_b")
-                    products = [acc, side_a, side_b]
+                    products = [acc, side_a]
 
                     def scalar_products(j, banks_j):
                         pixels = slice(j * BAND * W, (j + 1) * BAND * W)
@@ -435,9 +432,6 @@ def tile_graphaugmentation_pa_t_kernel(tc, x, mw, mb, attn_w, out):
                                     bias=bias[:, column : column + 1] if i == 0 else 0.0,
                                     scale=weight_of(i, b),
                                 )
-                        nc.gpsimd.tensor_tensor(
-                            out=side_a[:, :, pixels], in0=side_a[:, :, pixels], in1=side_b[:, :, pixels], op=ADD
-                        )
 
                     def vector_adds(j, source_banks, source_step):
                         pixels = slice(j * BAND * W, (j + 1) * BAND * W)

@@ -34,6 +34,7 @@ WORDS = 1536
 QUANT_WIDTHS = (4096, 2048)
 REGROUP_ROWS = 6
 REGROUP_STEPS = ROWS // REGROUP_ROWS
+EARLY = 2
 SCALAR_TAPS = 2
 
 MATRIX = B - LOOPED
@@ -43,7 +44,7 @@ MIXED = [i for i in range(TAPS) if abs(OFFSETS[i][0]) == GROUPS // 2]
 MOVED = [i for i in range(TAPS) if i not in MIXED]
 LOTS = MATRIX * PAIRS
 BLOCKS_A_TURN = 3
-FIRST_BLOCK = 6
+FIRST_BLOCK = 7
 PRODUCT_ENGINES = ("gpsimd", "gpsimd", "gpsimd", "scalar")
 
 
@@ -68,14 +69,16 @@ def tile_graphaugmentation_pa_t_kernel(tc, x, mw, mb, attn_w, out):
         nc.sync.dma_start(out=mb_rows[0:D_TILES, :], in_=mb.rearrange("(t p) -> t p", p=P))
         raw_tiles = {}
 
-        def load_looped(b, between=None):
+        def load_looped(b, cuts=()):
             raw = raws.tile([P, PACK, ROWS * W], BF16, name="raw")
             xb = x[b].rearrange("(p t) h w -> p t (h w)", t=PACK)
-            first = (H - ROW0) * W
-            nc.sync.dma_start(out=raw[:, :, 0:first], in_=xb[:, :, ROW0 * W : H * W])
-            if between is not None:
-                between()
-            nc.sync.dma_start(out=raw[:, :, first : ROWS * W], in_=xb[:, :, 0 : ROWS * W - first])
+            wrap = H - ROW0
+            cuts = [0, *cuts, wrap, ROWS]
+            for start, end in zip(cuts[:-1], cuts[1:]):
+                row = (start + ROW0) % H
+                nc.sync.dma_start(
+                    out=raw[:, :, start * W : end * W], in_=xb[:, :, row * W : (row + end - start) * W]
+                )
             raw_tiles[b] = raw
 
         def load_matrix(a):
@@ -83,13 +86,11 @@ def tile_graphaugmentation_pa_t_kernel(tc, x, mw, mb, attn_w, out):
             nc.sync.dma_start(out=raw[:], in_=x[LOOPED + a].rearrange("(p t) h w -> p t (h w)", t=PACK))
             raw_tiles[LOOPED + a] = raw
 
-        def load_mw():
-            nc.sync.dma_start(
-                out=mw_sb.rearrange("p (t c) -> p t c", t=D_TILES),
-                in_=mw.rearrange("(t p) c -> p t c", p=P),
-            )
-
-        load_looped(0, load_mw)
+        nc.sync.dma_start(
+            out=mw_sb.rearrange("p (t c) -> p t c", t=D_TILES),
+            in_=mw.rearrange("(t p) c -> p t c", p=P),
+        )
+        load_looped(0, [3 * REGROUP_ROWS])
         load_matrix(0)
         load_looped(1)
         load_looped(2)
@@ -168,17 +169,19 @@ def tile_graphaugmentation_pa_t_kernel(tc, x, mw, mb, attn_w, out):
 
         mixes = [const.tile([P, GROUP_ROWS + 1, W], F32, name="mix%d" % a) for a in range(MATRIX)]
 
+        mix_part = const.tile([P, GROUP_ROWS + 1, W], F32, name="mix_part")
+
         def build_mix(a):
             for i in MIXED:
                 dy, dx = OFFSETS[i]
                 row = 1 + source(dy, 0)[1]
                 part = ident_wide[:, row : row + GROUP_ROWS + 1, PAD - dx : PAD - dx + W]
-                if i == MIXED[0]:
-                    nc.vector.tensor_scalar_mul(out=mixes[a][:], in0=part, scalar1=weight_of(i, LOOPED + a))
-                else:
-                    nc.vector.scalar_tensor_tensor(
-                        out=mixes[a][:], in0=part, scalar=weight_of(i, LOOPED + a), in1=mixes[a][:], op0=MULT, op1=ADD
-                    )
+                share = mixes[a] if i == MIXED[0] else mix_part
+                nc.gpsimd.tensor_scalar(
+                    out=share[:], in0=part, scalar1=weight_of(i, LOOPED + a), scalar2=0.0, op0=MULT, op1=ADD
+                )
+                if i != MIXED[0]:
+                    nc.gpsimd.tensor_tensor(out=mixes[a][:], in0=mixes[a][:], in1=mix_part[:], op=ADD)
 
         m_grouped = const.tile([P, H * W * PACK], BF16, name="m_grouped", align_bytes=64)
         m_codes = [const.tile([P, H * W], U32, name="m_codes%d" % s, align_bytes=64) for s in range(2)]
@@ -225,12 +228,13 @@ def tile_graphaugmentation_pa_t_kernel(tc, x, mw, mb, attn_w, out):
                 )
 
             build_moves()
-            build_mix(0)
+            for a in range(MATRIX):
+                build_mix(a)
 
             third = WORDS * PACK // 3
-            for step in (0, 1, 2, 3, 4):
-                regroup(nc.scalar.copy if step % 3 == 2 else nc.vector.tensor_copy, 0, step)
-            quantise(0, (third,), 0)
+            regroup(nc.vector.tensor_copy, 0, 0)
+            regroup(nc.vector.tensor_copy, 0, 1)
+            regroup(nc.scalar.copy, 0, 2)
 
             for pair in range(PAIRS):
                 mw_t = prep.tile([P, PAIR, 2, P], F32, name="mw_t%d" % pair)
@@ -246,14 +250,18 @@ def tile_graphaugmentation_pa_t_kernel(tc, x, mw, mb, attn_w, out):
                     out=mw_grouped32[:, pair * PAIR : (pair + 1) * PAIR],
                     in_=mw_t.rearrange("p s u d -> p s d u"),
                 )
-            regroup(nc.scalar.copy, 0, 5)
             nc.vector.quantize_mx(
                 out=mw_codes[:].bitcast(FP8X4), scales=mw_scales[:], in_=mw_grouped[:]
             )
+            quantise(0, (third,), 0)
+            regroup(nc.vector.tensor_copy, 0, 3)
+            regroup(nc.vector.tensor_copy, 0, 4)
+            regroup(nc.vector.tensor_copy, 0, 5)
             quantise(0, (third, third), third)
 
-            for r in range(GROUPS):
+            for r in range(GROUPS // 2):
                 matrix_regroup_gpsimd(0, r)
+                matrix_regroup(0, GROUPS // 2 + r)
 
         load_looped(4)
         load_matrix(2)
@@ -297,7 +305,11 @@ def tile_graphaugmentation_pa_t_kernel(tc, x, mw, mb, attn_w, out):
                 scale = weight_of(MOVED[e], LOOPED + lot // PAIRS)
                 engine = PRODUCT_ENGINES[e]
                 if engine == "gpsimd":
-                    nc.gpsimd.tensor_scalar(out=product[:], in0=m, scalar1=scale, scalar2=0.0, op0=MULT, op1=ADD)
+                    for part in range(2):
+                        groups = slice(part * GROUPS // 2, (part + 1) * GROUPS // 2)
+                        nc.gpsimd.tensor_scalar(
+                            out=product[:, groups], in0=m[:, groups], scalar1=scale, scalar2=0.0, op0=MULT, op1=ADD
+                        )
                 else:
                     nc.scalar.activation(out=product[:], in_=m, func=IDENTITY, bias=0.0, scale=scale)
 
@@ -369,9 +381,7 @@ def tile_graphaugmentation_pa_t_kernel(tc, x, mw, mb, attn_w, out):
                         if a > 0 and base - 9 <= turn < base - 7:
                             for r in range(GROUPS // 2):
                                 matrix_regroup(a, r + (turn - base + 9) * GROUPS // 2)
-                        if turn == base - 10 and a > 0:
-                            build_mix(a)
-                        if turn == max(base - 7, 1):
+                        if turn == max(base - 7, 2):
                             matrix_quantise(a)
                     if turn == base - 4:
                         messages = [(q, u) for u in range(GROUPS // 2)]
@@ -484,10 +494,10 @@ def tile_graphaugmentation_pa_t_kernel(tc, x, mw, mb, attn_w, out):
                             regroup(nc.scalar.copy, 1, step)
                         if b == 0 and step == REGROUP_STEPS - 1:
                             quantise(1)
-                        if b + 2 < LOOPED and step == 2 * BANDS - 1:
-                            regroup(nc.scalar.copy, b + 2, 0)
-                        if 0 < b and b + 1 < LOOPED and step < REGROUP_STEPS - 1:
-                            regroup(nc.scalar.copy, b + 1, step + 1)
+                        if b + 2 < LOOPED and step >= 2 * BANDS - EARLY:
+                            regroup(nc.scalar.copy, b + 2, step - 2 * BANDS + EARLY)
+                        if 0 < b and b + 1 < LOOPED and step < REGROUP_STEPS - EARLY:
+                            regroup(nc.scalar.copy, b + 1, step + EARLY)
                         if 0 < b and b + 1 < LOOPED and step == REGROUP_STEPS - 2:
                             quantise(b + 1)
                     vector_adds(0, before, -1)

@@ -420,87 +420,108 @@ def tile_graphaugmentation_pa_t_kernel(tc, x, mw, mb, attn_w, out):
                 pair, j = divmod(rest, BANDS)
                 return [fill(b, pair * PAIR + s, j) for s in range(PAIR)]
 
-            ahead = fills(0)
-            for b in range(LOOPED):
-                for pair in range(PAIRS):
-                    d_tiles = [pair * PAIR + s for s in range(PAIR)]
-                    acc = accs.tile([P, PAIR, H * W], F32, name="acc")
-                    side_a = sides.tile([P, PAIR, H * W], F32, name="side_a")
-                    products = [acc, side_a]
+            parts = {}
 
-                    def scalar_products(j, banks_j):
-                        pixels = slice(j * BAND * W, (j + 1) * BAND * W)
-                        for i in reversed(range(SCALAR_TAPS)):
-                            bank_step, row, col = tap_window(*OFFSETS[i])
-                            assert bank_step == 0
-                            for s in range(PAIR):
-                                column = d_tiles[s] * B + b
-                                nc.scalar.activation(
-                                    out=products[i][:, s, pixels].rearrange("p (r c) -> p r c", c=W),
-                                    in_=banks_j[s][:, row : row + BAND, col : col + W],
-                                    func=IDENTITY,
-                                    bias=bias[:, column : column + 1] if i == 0 else 0.0,
-                                    scale=weight_of(i, b),
-                                )
+            def parts_of(turn):
+                pair = turn // BANDS
+                if pair not in parts:
+                    parts[pair] = (
+                        accs.tile([P, PAIR, H * W], F32, name="acc"),
+                        sides.tile([P, PAIR, H * W], F32, name="side_a"),
+                        sides.tile([P, PAIR, H * W], F32, name="side_b"),
+                    )
+                return parts[pair]
 
-                    def vector_adds(j, source_banks, source_step):
-                        pixels = slice(j * BAND * W, (j + 1) * BAND * W)
-                        for i in range(SCALAR_TAPS, TAPS):
-                            bank_step, row, col = tap_window(*OFFSETS[i])
-                            if bank_step != source_step:
-                                continue
-                            for s in range(PAIR):
-                                band = acc[:, s, pixels].rearrange("p (r c) -> p r c", c=W)
-                                nc.vector.scalar_tensor_tensor(
-                                    out=band,
-                                    in0=source_banks[s][:, row : row + BAND, col : col + W],
-                                    scalar=weight_of(i, b),
-                                    in1=band,
-                                    op0=MULT,
-                                    op1=ADD,
-                                )
+            def scalar_taps(turn):
+                return 3 if turn % BANDS == BANDS - 1 else 2
 
-                    def finish(j):
-                        pixels = slice(j * BAND * W, (j + 1) * BAND * W)
-                        last = b == LOOPED - 1 and pair == PAIRS - 1 and j == 0
-                        (nc.vector if last else nc.gpsimd).tensor_tensor(
-                            out=acc[:, :, pixels], in0=acc[:, :, pixels], in1=side_a[:, :, pixels], op=ADD
-                        )
-                        nc.sync.dma_start(
-                            out=out[
-                                b, pair * PAIR * P : (pair + 1) * PAIR * P, j * BAND : (j + 1) * BAND, :
-                            ].rearrange("(s p) r w -> p s (r w)", p=P),
-                            in_=acc[:, :, pixels],
+            def pixels_of(turn):
+                return slice(turn % BANDS * BAND * W, (turn % BANDS + 1) * BAND * W)
+
+            def scalar_products(turn, banks_j):
+                b, pair = divmod(turn // BANDS, PAIRS)
+                pixels = pixels_of(turn)
+                for i in reversed(range(scalar_taps(turn))):
+                    bank_step, row, col = tap_window(*OFFSETS[i])
+                    assert bank_step == 0
+                    for s in range(PAIR):
+                        column = (pair * PAIR + s) * B + b
+                        nc.scalar.activation(
+                            out=parts_of(turn)[i][:, s, pixels].rearrange("p (r c) -> p r c", c=W),
+                            in_=banks_j[s][:, row : row + BAND, col : col + W],
+                            func=IDENTITY,
+                            bias=bias[:, column : column + 1] if i == 0 else 0.0,
+                            scale=weight_of(i, b),
                         )
 
-                    before = None
-                    for j in range(BANDS):
-                        here = ahead
-                        scalar_products(j, here)
-                        if j > 0:
-                            vector_adds(j, before, -1)
-                        while leaving:
-                            matrix_leave()
-                        turn = (b * PAIRS + pair) * BANDS + j
-                        if turn + 1 < LOOPED * PAIRS * BANDS:
-                            ahead = fills(turn + 1)
-                        matrix_turn(turn)
-                        vector_adds(j, here, 0)
-                        if j > 0:
-                            finish(j)
-                        before = here
-                        step = pair * BANDS + j
-                        if b == 0 and step < REGROUP_STEPS:
-                            regroup(nc.scalar.copy, 1, step)
-                        if b == 0 and step == REGROUP_STEPS - 1:
-                            quantise(1)
-                        if b + 2 < LOOPED and step >= 2 * BANDS - EARLY:
-                            regroup(nc.scalar.copy, b + 2, step - 2 * BANDS + EARLY)
-                        if 0 < b and b + 1 < LOOPED and step < REGROUP_STEPS - EARLY:
-                            regroup(nc.scalar.copy, b + 1, step + EARLY)
-                        if 0 < b and b + 1 < LOOPED and step == REGROUP_STEPS - 2:
-                            quantise(b + 1)
-                    vector_adds(0, before, -1)
-                    finish(0)
+            def early_join(turn):
+                if scalar_taps(turn) == 3:
+                    acc, side_a, side_b = parts_of(turn)
+                    pixels = pixels_of(turn)
+                    nc.gpsimd.tensor_tensor(
+                        out=side_a[:, :, pixels], in0=side_a[:, :, pixels], in1=side_b[:, :, pixels], op=ADD
+                    )
+
+            def vector_adds(turn, source_banks, source_step):
+                b = turn // (PAIRS * BANDS)
+                for i in range(scalar_taps(turn), TAPS):
+                    bank_step, row, col = tap_window(*OFFSETS[i])
+                    if bank_step != source_step:
+                        continue
+                    for s in range(PAIR):
+                        band = parts_of(turn)[0][:, s, pixels_of(turn)].rearrange("p (r c) -> p r c", c=W)
+                        nc.vector.scalar_tensor_tensor(
+                            out=band,
+                            in0=source_banks[s][:, row : row + BAND, col : col + W],
+                            scalar=weight_of(i, b),
+                            in1=band,
+                            op0=MULT,
+                            op1=ADD,
+                        )
+
+            def finish(turn, engine):
+                b, pair = divmod(turn // BANDS, PAIRS)
+                acc, side_a, side_b = parts_of(turn)
+                pixels = pixels_of(turn)
+                engine.tensor_tensor(out=acc[:, :, pixels], in0=acc[:, :, pixels], in1=side_a[:, :, pixels], op=ADD)
+                j = turn % BANDS
+                nc.sync.dma_start(
+                    out=out[b, pair * PAIR * P : (pair + 1) * PAIR * P, j * BAND : (j + 1) * BAND, :].rearrange(
+                        "(s p) r w -> p s (r w)", p=P
+                    ),
+                    in_=acc[:, :, pixels],
+                )
+
+            turns = LOOPED * PAIRS * BANDS
+            filled = {0: fills(0)}
+            scalar_products(0, filled[0])
+            for turn in range(turns):
+                b, step = divmod(turn, PAIRS * BANDS)
+                j = turn % BANDS
+                early_join(turn)
+                if j > 0:
+                    vector_adds(turn, filled[turn - 1], -1)
+                while leaving:
+                    matrix_leave()
+                if turn + 1 < turns:
+                    filled[turn + 1] = fills(turn + 1)
+                    scalar_products(turn + 1, filled[turn + 1])
+                matrix_turn(turn)
+                vector_adds(turn, filled[turn], 0)
+                if j > 0:
+                    finish(turn, nc.gpsimd)
+                if b == 0 and step < REGROUP_STEPS:
+                    regroup(nc.scalar.copy, 1, step)
+                if b == 0 and step == REGROUP_STEPS - 1:
+                    quantise(1)
+                if b + 2 < LOOPED and step >= 2 * BANDS - EARLY:
+                    regroup(nc.scalar.copy, b + 2, step - 2 * BANDS + EARLY)
+                if 0 < b and b + 1 < LOOPED and step < REGROUP_STEPS - EARLY:
+                    regroup(nc.scalar.copy, b + 1, step + EARLY)
+                if 0 < b and b + 1 < LOOPED and step == REGROUP_STEPS - 2:
+                    quantise(b + 1)
+                if j == BANDS - 1:
+                    vector_adds(turn - j, filled[turn], -1)
+                    finish(turn - j, nc.vector if turn == turns - 1 else nc.gpsimd)
             while leaving:
                 matrix_leave()

@@ -69,7 +69,7 @@ def tile_graphaugmentation_pa_t_kernel(tc, x, mw, mb, attn_w, out):
         nc.sync.dma_start(out=mb_rows[0:D_TILES, :], in_=mb.rearrange("(t p) -> t p", p=P))
         raw_tiles = {}
 
-        def load_looped(b, cuts=()):
+        def load_looped(b, cuts=(), after_first=None):
             raw = raws.tile([P, PACK, ROWS * W], BF16, name="raw")
             xb = x[b].rearrange("(p t) h w -> p t (h w)", t=PACK)
             wrap = H - ROW0
@@ -79,6 +79,8 @@ def tile_graphaugmentation_pa_t_kernel(tc, x, mw, mb, attn_w, out):
                 nc.sync.dma_start(
                     out=raw[:, :, start * W : end * W], in_=xb[:, :, row * W : (row + end - start) * W]
                 )
+                if start == 0 and after_first is not None:
+                    after_first()
             raw_tiles[b] = raw
 
         def load_matrix(a):
@@ -86,13 +88,17 @@ def tile_graphaugmentation_pa_t_kernel(tc, x, mw, mb, attn_w, out):
             nc.sync.dma_start(out=raw[:], in_=x[LOOPED + a].rearrange("(p t) h w -> p t (h w)", t=PACK))
             raw_tiles[LOOPED + a] = raw
 
-        nc.sync.dma_start(
-            out=mw_sb.rearrange("p (t c) -> p t c", t=D_TILES),
-            in_=mw.rearrange("(t p) c -> p t c", p=P),
-        )
-        load_looped(0, [3 * REGROUP_ROWS])
-        load_matrix(0)
+        def load_mw(pair):
+            tiles = slice(pair * PAIR, (pair + 1) * PAIR)
+            nc.sync.dma_start(
+                out=mw_sb.rearrange("p (t c) -> p t c", t=D_TILES)[:, tiles],
+                in_=mw.rearrange("(t p) c -> p t c", p=P)[:, tiles],
+            )
+
+        load_mw(0)
+        load_looped(0, [3 * REGROUP_ROWS], lambda: load_mw(1))
         load_looped(1)
+        load_matrix(0)
         load_looped(2)
         load_matrix(1)
         load_looped(3)
@@ -156,16 +162,16 @@ def tile_graphaugmentation_pa_t_kernel(tc, x, mw, mb, attn_w, out):
             for carry in sorted({source(OFFSETS[i][0], r)[1] for r in range(GROUPS)}):
                 moves[i, carry] = const.tile([P, GROUP_ROWS, W], F32, name="move%d_%d" % (i, carry + 1))
 
-        def build_moves():
+        def build_moves(copy):
             inner = slice(1, 1 + GROUP_ROWS)
-            nc.vector.tensor_copy(out=ident_wide[:, inner, PAD : PAD + W], in_=ident_rows)
-            nc.vector.tensor_copy(out=ident_wide[:, inner, 0:PAD], in_=ident_rows[:, :, W - PAD : W])
-            nc.vector.tensor_copy(out=ident_wide[:, inner, PAD + W : PITCH], in_=ident_rows[:, :, 0:PAD])
-            nc.vector.tensor_copy(out=ident_wide[:, 0, :], in_=ident_wide[:, GROUP_ROWS, :])
-            nc.vector.tensor_copy(out=ident_wide[:, GROUP_ROWS + 1, :], in_=ident_wide[:, 1, :])
+            copy(out=ident_wide[:, inner, PAD : PAD + W], in_=ident_rows)
+            copy(out=ident_wide[:, inner, 0:PAD], in_=ident_rows[:, :, W - PAD : W])
+            copy(out=ident_wide[:, inner, PAD + W : PITCH], in_=ident_rows[:, :, 0:PAD])
+            copy(out=ident_wide[:, 0, :], in_=ident_wide[:, GROUP_ROWS, :])
+            copy(out=ident_wide[:, GROUP_ROWS + 1, :], in_=ident_wide[:, 1, :])
             for (i, carry), move in moves.items():
                 cols = slice(PAD - OFFSETS[i][1], PAD - OFFSETS[i][1] + W)
-                nc.vector.tensor_copy(out=move[:], in_=ident_wide[:, 1 + carry : 1 + carry + GROUP_ROWS, cols])
+                copy(out=move[:], in_=ident_wide[:, 1 + carry : 1 + carry + GROUP_ROWS, cols])
 
         mixes = [const.tile([P, GROUP_ROWS + 1, W], F32, name="mix%d" % a) for a in range(MATRIX)]
 
@@ -214,8 +220,9 @@ def tile_graphaugmentation_pa_t_kernel(tc, x, mw, mb, attn_w, out):
         mw_grouped32 = mw_grouped[:].bitcast(F32).rearrange("p (t d u) -> p t d u", t=D_TILES, u=2)
         mw_codes = const.tile([P, C], U32, name="mw_codes", align_bytes=64)
         mw_scales = const.tile([P, C], U8, name="mw_scales", align_bytes=64)
-        with tc.psum_pool(name="prep", bufs=1) as prep:
-            mb_t = prep.tile([P, P], F32, name="mb_t")
+        with tc.psum_pool(name="banks", bufs=6) as banks, tc.psum_pool(name="m_banks", bufs=2) as m_banks:
+            build_moves(nc.scalar.copy)
+            mb_t = m_banks.tile([P, P], F32, name="m_bank")
             nc.tensor.transpose(mb_t[:], mb_rows32[:], ident[:])
             nc.scalar.copy(out=mb_col[:], in_=mb_t[:, 0:D_TILES])
             for t in range(D_TILES):
@@ -227,17 +234,8 @@ def tile_graphaugmentation_pa_t_kernel(tc, x, mw, mb, attn_w, out):
                     scale=mb_col[:, t : t + 1],
                 )
 
-            build_moves()
-            for a in range(MATRIX):
-                build_mix(a)
-
-            third = WORDS * PACK // 3
-            regroup(nc.vector.tensor_copy, 0, 0)
-            regroup(nc.vector.tensor_copy, 0, 1)
-            regroup(nc.scalar.copy, 0, 2)
-
-            for pair in range(PAIRS):
-                mw_t = prep.tile([P, PAIR, 2, P], F32, name="mw_t%d" % pair)
+            def prepare_mw(pair):
+                mw_t = m_banks.tile([P, PAIR, 2, P], F32, name="m_bank")
                 for s in range(PAIR):
                     t = pair * PAIR + s
                     for u in range(2):
@@ -246,27 +244,29 @@ def tile_graphaugmentation_pa_t_kernel(tc, x, mw, mb, attn_w, out):
                             mw_words32[:, t * half_c + u : (t + 1) * half_c : 2],
                             ident[:],
                         )
-                (nc.vector.tensor_copy if pair == 0 else nc.scalar.copy)(
+                nc.scalar.copy(
                     out=mw_grouped32[:, pair * PAIR : (pair + 1) * PAIR],
                     in_=mw_t.rearrange("p s u d -> p s d u"),
                 )
-            nc.vector.quantize_mx(
-                out=mw_codes[:].bitcast(FP8X4), scales=mw_scales[:], in_=mw_grouped[:]
-            )
+
+            def quantise_mw(pair):
+                d_cols = slice(pair * PAIR * P, (pair + 1) * PAIR * P)
+                nc.vector.quantize_mx(
+                    out=mw_codes[:, d_cols].bitcast(FP8X4),
+                    scales=mw_scales[:, d_cols],
+                    in_=mw_grouped[:, pair * PAIR * P * PACK : (pair + 1) * PAIR * P * PACK],
+                )
+
+            third = WORDS * PACK // 3
+            prepare_mw(0)
+            quantise_mw(0)
+            regroup(nc.vector.tensor_copy, 0, 0)
+            regroup(nc.vector.tensor_copy, 0, 1)
+            regroup(nc.scalar.copy, 0, 2)
             quantise(0, (third,), 0)
             regroup(nc.vector.tensor_copy, 0, 3)
-            regroup(nc.vector.tensor_copy, 0, 4)
-            regroup(nc.vector.tensor_copy, 0, 5)
-            quantise(0, (third, third), third)
-
-            for r in range(GROUPS // 2):
-                matrix_regroup_gpsimd(0, r)
-                matrix_regroup(0, GROUPS // 2 + r)
-
-        load_looped(4)
-        load_matrix(2)
-
-        with tc.psum_pool(name="banks", bufs=6) as banks, tc.psum_pool(name="m_banks", bufs=2) as m_banks:
+            regroup(nc.scalar.copy, 0, 4)
+            quantise(0, (third,), third)
 
             m_tiles = {}
             m_products = {}
@@ -378,11 +378,12 @@ def tile_graphaugmentation_pa_t_kernel(tc, x, mw, mb, attn_w, out):
                     base = FIRST_BLOCK + 2 * GROUPS * q // BLOCKS_A_TURN
                     a, pair = divmod(q, PAIRS)
                     if pair == 0:
-                        if a > 0 and base - 9 <= turn < base - 7:
-                            for r in range(GROUPS // 2):
-                                matrix_regroup(a, r + (turn - base + 9) * GROUPS // 2)
-                        if turn == max(base - 7, 2):
-                            matrix_quantise(a)
+                        for start, per, done in ((-9, 8, 2), (3, 2, 7), (9, 1, 17))[a : a + 1]:
+                            for r in range(GROUPS):
+                                if turn == start + r // per:
+                                    matrix_regroup(a, r)
+                            if turn == done:
+                                matrix_quantise(a)
                     if turn == base - 4:
                         messages = [(q, u) for u in range(GROUPS // 2)]
                 first = (turn - FIRST_BLOCK) * BLOCKS_A_TURN
@@ -433,7 +434,7 @@ def tile_graphaugmentation_pa_t_kernel(tc, x, mw, mb, attn_w, out):
                 return parts[pair]
 
             def scalar_taps(turn):
-                return 3 if turn % BANDS == BANDS - 1 else 2
+                return 3 if turn >= 24 and turn % 2 == 1 else 2
 
             def pixels_of(turn):
                 return slice(turn % BANDS * BAND * W, (turn % BANDS + 1) * BAND * W)
@@ -495,6 +496,13 @@ def tile_graphaugmentation_pa_t_kernel(tc, x, mw, mb, attn_w, out):
             turns = LOOPED * PAIRS * BANDS
             filled = {0: fills(0)}
             scalar_products(0, filled[0])
+            prepare_mw(1)
+            regroup(nc.scalar.copy, 0, 5)
+            load_looped(4)
+            for r in range(GROUPS // 2):
+                matrix_regroup_gpsimd(0, r)
+            for a in range(MATRIX):
+                build_mix(a)
             for turn in range(turns):
                 b, step = divmod(turn, PAIRS * BANDS)
                 j = turn % BANDS
@@ -510,6 +518,12 @@ def tile_graphaugmentation_pa_t_kernel(tc, x, mw, mb, attn_w, out):
                 vector_adds(turn, filled[turn], 0)
                 if j > 0:
                     finish(turn, nc.gpsimd)
+                if turn == 0:
+                    quantise(0, (third,), 2 * third)
+                    quantise_mw(1)
+                    for r in range(GROUPS // 2):
+                        matrix_regroup(0, GROUPS // 2 + r)
+                    load_matrix(2)
                 if b == 0 and step < REGROUP_STEPS:
                     regroup(nc.scalar.copy, 1, step)
                 if b == 0 and step == REGROUP_STEPS - 1:

import concourse.mybir as mybir
from concourse.masks import make_identity

F32 = mybir.dt.float32
BF16 = mybir.dt.bfloat16
U32 = mybir.dt.uint32
U8 = mybir.dt.uint8
FP8X4 = mybir.dt.float8_e4m3fn_x4
MULT = mybir.AluOpType.mult
ADD = mybir.AluOpType.add
IDENTITY = mybir.ActivationFunctionType.Identity

B, C, H, W = 8, 512, 32, 32
OFFSETS = [(-4, -4), (-4, -1), (-4, 2), (-3, 4), (-2, -3), (2, 3), (3, -2), (4, 4)]
TAPS = len(OFFSETS)
FLOPS = 2 * B * C * C * H * W + 2 * TAPS * B * C * H * W

P = 128
PACK = 4
D_TILES = C // P
PAIR = 2
PAIRS = D_TILES // PAIR

LOOPED = 5
PAD = 4
PITCH = W + 2 * PAD
ROW0 = 2
BAND = 8
BANDS = H // BAND
BANK_COLS = 512
BANK_ROWS = BANK_COLS // PITCH
ROWS = (BANDS - 1) * BAND + BANK_ROWS
WORDS = 1536
QUANT_WIDTHS = (4096, 2048)
REGROUP_ROWS = 6
REGROUP_STEPS = ROWS // REGROUP_ROWS
EARLY = 2
SCALAR_TAPS = 2

MATRIX = B - LOOPED
GROUPS = 8
GROUP_ROWS = H // GROUPS
MIXED = [i for i in range(TAPS) if abs(OFFSETS[i][0]) == GROUPS // 2]
MOVED = [i for i in range(TAPS) if i not in MIXED]
LOTS = MATRIX * PAIRS
BLOCKS_A_TURN = 3
FIRST_BLOCK = 7
PRODUCT_ENGINES = ("gpsimd", "gpsimd", "gpsimd", "scalar")


def tap_window(dy, dx):
    bank_step, first_row = divmod(-dy - ROW0, BAND)
    assert bank_step in (-1, 0) and first_row + BAND <= BANK_ROWS
    return bank_step, first_row, PAD - dx


def tile_graphaugmentation_pa_t_kernel(tc, x, mw, mb, attn_w, out):
    nc = tc.nc
    with tc.manual_schedule(), tc.tile_pool(name="const", bufs=1) as const, tc.tile_pool(
        name="raws", bufs=4
    ) as raws, tc.tile_pool(name="m_raws", bufs=2) as m_raws, tc.tile_pool(name="accs", bufs=3) as accs, tc.tile_pool(
        name="sides", bufs=2
    ) as sides, tc.tile_pool(name="m_work", bufs=2) as m_work:
        mw_sb = const.tile([P, D_TILES * C], BF16, name="mw_sb")
        w_bf = const.tile([P, TAPS * B], BF16, name="w_bf")
        nc.sync.dma_start(out=w_bf[:], in_=attn_w.rearrange("i b -> (i b)").partition_broadcast(P))
        mb_rows = const.tile([P, P], BF16, name="mb_rows")
        nc.vector.memset(mb_rows[:], 0.0)
        nc.sync.dma_start(out=mb_rows[0:D_TILES, :], in_=mb.rearrange("(t p) -> t p", p=P))
        raw_tiles = {}

        def load_looped(b, cuts=(), after_first=None):
            raw = raws.tile([P, PACK, ROWS * W], BF16, name="raw")
            xb = x[b].rearrange("(p t) h w -> p t (h w)", t=PACK)
            wrap = H - ROW0
            cuts = [0, *cuts, wrap, ROWS]
            for start, end in zip(cuts[:-1], cuts[1:]):
                row = (start + ROW0) % H
                nc.sync.dma_start(
                    out=raw[:, :, start * W : end * W], in_=xb[:, :, row * W : (row + end - start) * W]
                )
                if start == 0 and after_first is not None:
                    after_first()
            raw_tiles[b] = raw

        def load_matrix(a):
            raw = m_raws.tile([P, PACK, H * W], BF16, name="m_raw")
            nc.sync.dma_start(out=raw[:], in_=x[LOOPED + a].rearrange("(p t) h w -> p t (h w)", t=PACK))
            raw_tiles[LOOPED + a] = raw

        def load_mw(pair):
            tiles = slice(pair * PAIR, (pair + 1) * PAIR)
            nc.sync.dma_start(
                out=mw_sb.rearrange("p (t c) -> p t c", t=D_TILES)[:, tiles],
                in_=mw.rearrange("(t p) c -> p t c", p=P)[:, tiles],
            )

        load_mw(0)
        load_looped(0, [3 * REGROUP_ROWS], lambda: load_mw(1))
        load_looped(1)
        load_matrix(0)
        load_looped(2)
        load_matrix(1)
        load_looped(3)

        ident = const.tile([P, P], F32, name="ident")
        make_identity(nc, ident[:])

        grouped = const.tile([P, WORDS * PACK], BF16, name="grouped", align_bytes=64)
        nc.vector.memset(grouped[:, ROWS * PITCH * PACK :], 0.0)
        grouped_blocks = grouped[:, 0 : ROWS * PITCH * PACK].rearrange(
            "p (r c i t) -> p r c t i", c=PITCH // PAD, i=PAD, t=PACK
        )
        x_codes = [const.tile([P, WORDS], U32, name="x_codes%d" % s, align_bytes=64) for s in range(2)]
        x_scales = [const.tile([P, WORDS], U8, name="x_scales%d" % s, align_bytes=64) for s in range(2)]

        def regroup(copy, b, step):
            rows = slice(step * REGROUP_ROWS, (step + 1) * REGROUP_ROWS)
            src = raw_tiles[b].rearrange("p t (r c i) -> p r c t i", c=W // PAD, i=PAD)
            last = W // PAD - 1
            copy(out=grouped_blocks[:, rows, 1 : 1 + W // PAD], in_=src[:, rows])
            copy(out=grouped_blocks[:, rows, 0], in_=src[:, rows, last])
            copy(out=grouped_blocks[:, rows, 1 + W // PAD], in_=src[:, rows, 0])

        def quantise(b, widths=QUANT_WIDTHS, start=0):
            for width in widths:
                words = slice(start // PACK, (start + width) // PACK)
                nc.vector.quantize_mx(
                    out=x_codes[b % 2][:, words].bitcast(FP8X4),
                    scales=x_scales[b % 2][:, words],
                    in_=grouped[:, start : start + width],
                )
                start += width

        weight = const.tile([P, TAPS * B], F32, name="weight")
        nc.vector.tensor_copy(out=weight[:], in_=w_bf[:])

        def weight_of(i, b):
            return weight[:, i * B + b : i * B + b + 1]

        weight_sum = const.tile([P, B], F32, name="weight_sum")
        nc.vector.tensor_reduce(
            out=weight_sum[:],
            in_=weight[:].rearrange("p (i b) -> p b i", b=B),
            axis=mybir.AxisListType.X,
            op=ADD,
        )
        mb_rows32 = const.tile([P, P], F32, name="mb_rows32")
        nc.vector.tensor_copy(out=mb_rows32[:], in_=mb_rows[:])
        mb_col = const.tile([P, D_TILES], F32, name="mb_col")
        bias = const.tile([P, D_TILES * B], F32, name="bias")

        ident_rows = ident.rearrange("p (k c) -> p k c", c=W)
        ident_wide = const.tile([P, GROUP_ROWS + 2, PITCH], F32, name="ident_wide")

        def source(dy, r):
            carry, group = divmod(r - dy, GROUPS)
            return group, carry

        moves = {}
        for i in MOVED:
            for carry in sorted({source(OFFSETS[i][0], r)[1] for r in range(GROUPS)}):
                moves[i, carry] = const.tile([P, GROUP_ROWS, W], F32, name="move%d_%d" % (i, carry + 1))

        def build_moves(copy):
            inner = slice(1, 1 + GROUP_ROWS)
            copy(out=ident_wide[:, inner, PAD : PAD + W], in_=ident_rows)
            copy(out=ident_wide[:, inner, 0:PAD], in_=ident_rows[:, :, W - PAD : W])
            copy(out=ident_wide[:, inner, PAD + W : PITCH], in_=ident_rows[:, :, 0:PAD])
            copy(out=ident_wide[:, 0, :], in_=ident_wide[:, GROUP_ROWS, :])
            copy(out=ident_wide[:, GROUP_ROWS + 1, :], in_=ident_wide[:, 1, :])
            for (i, carry), move in moves.items():
                cols = slice(PAD - OFFSETS[i][1], PAD - OFFSETS[i][1] + W)
                copy(out=move[:], in_=ident_wide[:, 1 + carry : 1 + carry + GROUP_ROWS, cols])

        mixes = [const.tile([P, GROUP_ROWS + 1, W], F32, name="mix%d" % a) for a in range(MATRIX)]

        mix_part = const.tile([P, GROUP_ROWS + 1, W], F32, name="mix_part")

        def build_mix(a):
            for i in MIXED:
                dy, dx = OFFSETS[i]
                row = 1 + source(dy, 0)[1]
                part = ident_wide[:, row : row + GROUP_ROWS + 1, PAD - dx : PAD - dx + W]
                share = mixes[a] if i == MIXED[0] else mix_part
                nc.gpsimd.tensor_scalar(
                    out=share[:], in0=part, scalar1=weight_of(i, LOOPED + a), scalar2=0.0, op0=MULT, op1=ADD
                )
                if i != MIXED[0]:
                    nc.gpsimd.tensor_tensor(out=mixes[a][:], in0=mixes[a][:], in1=mix_part[:], op=ADD)

        m_grouped = const.tile([P, H * W * PACK], BF16, name="m_grouped", align_bytes=64)
        m_codes = [const.tile([P, H * W], U32, name="m_codes%d" % s, align_bytes=64) for s in range(2)]
        m_scales = [const.tile([P, H * W], U8, name="m_scales%d" % s, align_bytes=64) for s in range(2)]

        def matrix_regroup_gpsimd(a, r):
            nc.gpsimd.tensor_scalar(
                out=m_grouped.rearrange("p (r k c t) -> p r k c t", r=GROUPS, c=W, t=PACK)[:, r],
                in0=raw_tiles[LOOPED + a].rearrange("p t (k r c) -> p r k c t", r=GROUPS, c=W)[:, r],
                scalar1=1.0,
                scalar2=0.0,
                op0=MULT,
                op1=ADD,
            )

        def matrix_regroup(a, r):
            nc.scalar.copy(
                out=m_grouped.rearrange("p (r k c i t) -> p r k c t i", r=GROUPS, c=W // PAD, i=PAD, t=PACK)[:, r],
                in_=raw_tiles[LOOPED + a].rearrange("p t (k r c i) -> p r k c t i", r=GROUPS, c=W // PAD, i=PAD)[:, r],
            )

        def matrix_quantise(a):
            nc.vector.quantize_mx(
                out=m_codes[a % 2][:].bitcast(FP8X4), scales=m_scales[a % 2][:], in_=m_grouped[:]
            )

        mw_words32 = mw_sb[:].bitcast(F32)
        half_c = C // 2
        mw_grouped = const.tile([P, C * PACK], BF16, name="mw_grouped", align_bytes=64)
        mw_grouped32 = mw_grouped[:].bitcast(F32).rearrange("p (t d u) -> p t d u", t=D_TILES, u=2)
        mw_codes = const.tile([P, C], U32, name="mw_codes", align_bytes=64)
        mw_scales = const.tile([P, C], U8, name="mw_scales", align_bytes=64)
        with tc.psum_pool(name="banks", bufs=6) as banks, tc.psum_pool(name="m_banks", bufs=2) as m_banks:
            build_moves(nc.scalar.copy)
            mb_t = m_banks.tile([P, P], F32, name="m_bank")
            nc.tensor.transpose(mb_t[:], mb_rows32[:], ident[:])
            nc.scalar.copy(out=mb_col[:], in_=mb_t[:, 0:D_TILES])
            for t in range(D_TILES):
                nc.scalar.activation(
                    out=bias[:, t * B : (t + 1) * B],
                    in_=weight_sum[:],
                    func=IDENTITY,
                    bias=0.0,
                    scale=mb_col[:, t : t + 1],
                )

            def prepare_mw(pair):
                mw_t = m_banks.tile([P, PAIR, 2, P], F32, name="m_bank")
                for s in range(PAIR):
                    t = pair * PAIR + s
                    for u in range(2):
                        nc.tensor.transpose(
                            mw_t[:, s, u, :],
                            mw_words32[:, t * half_c + u : (t + 1) * half_c : 2],
                            ident[:],
                        )
                nc.scalar.copy(
                    out=mw_grouped32[:, pair * PAIR : (pair + 1) * PAIR],
                    in_=mw_t.rearrange("p s u d -> p s d u"),
                )

            def quantise_mw(pair):
                d_cols = slice(pair * PAIR * P, (pair + 1) * PAIR * P)
                nc.vector.quantize_mx(
                    out=mw_codes[:, d_cols].bitcast(FP8X4),
                    scales=mw_scales[:, d_cols],
                    in_=mw_grouped[:, pair * PAIR * P * PACK : (pair + 1) * PAIR * P * PACK],
                )

            third = WORDS * PACK // 3
            prepare_mw(0)
            quantise_mw(0)
            regroup(nc.vector.tensor_copy, 0, 0)
            regroup(nc.vector.tensor_copy, 0, 1)
            regroup(nc.scalar.copy, 0, 2)
            quantise(0, (third,), 0)
            regroup(nc.vector.tensor_copy, 0, 3)
            regroup(nc.scalar.copy, 0, 4)
            quantise(0, (third,), third)

            m_tiles = {}
            m_products = {}
            m_holders = []
            leaving = []

            def m_bank(holder):
                m_holders.append(holder)
                if len(m_holders) > 2 and m_holders[-3] in leaving:
                    matrix_leave()
                return m_banks.tile([P, 2, PAIR * P], F32, name="m_bank")

            def matrix_messages(lot, u):
                a, pair = divmod(lot, PAIRS)
                if u == 0:
                    m_tiles[lot] = m_work.tile([P, GROUPS, PAIR * P], F32, name="m_tile")
                bank = m_bank(None)
                d_cols = slice(pair * PAIR * P, (pair + 1) * PAIR * P)
                for v in range(2):
                    cols = slice((2 * u + v) * P, (2 * u + v + 1) * P)
                    nc.tensor.matmul_mx(
                        out=bank[:, v, :],
                        lhsT=m_codes[a % 2][:, cols].bitcast(FP8X4),
                        lhsT_scale=m_scales[a % 2][:, cols],
                        rhs=mw_codes[:, d_cols].bitcast(FP8X4),
                        rhs_scale=mw_scales[:, d_cols],
                        start=True,
                        stop=True,
                    )
                nc.scalar.copy(out=m_tiles[lot][:, 2 * u : 2 * u + 2, :], in_=bank[:])

            def matrix_product(lot, s, e):
                product = m_work.tile([P, GROUPS, P], F32, name="m_product%d" % e)
                m_products[lot, s, e] = product
                m = m_tiles[lot][:, :, s * P : (s + 1) * P]
                scale = weight_of(MOVED[e], LOOPED + lot // PAIRS)
                engine = PRODUCT_ENGINES[e]
                if engine == "gpsimd":
                    for part in range(2):
                        groups = slice(part * GROUPS // 2, (part + 1) * GROUPS // 2)
                        nc.gpsimd.tensor_scalar(
                            out=product[:, groups], in0=m[:, groups], scalar1=scale, scalar2=0.0, op0=MULT, op1=ADD
                        )
                else:
                    nc.scalar.activation(out=product[:], in_=m, func=IDENTITY, bias=0.0, scale=scale)

            m_sums = {}

            def matrix_block(lot, s, r):
                half, place = divmod(r, GROUPS // 2)
                if place == 0:
                    m_sums[lot, s, half] = m_bank((lot, s, half)).rearrange("p v d -> p (v d)")
                pixels = m_sums[lot, s, half][:, place * P : (place + 1) * P]

                def mixed(start):
                    group, carry = source(-(GROUPS // 2), r)
                    nc.tensor.matmul(
                        out=pixels,
                        lhsT=m_tiles[lot][:, group, s * P : (s + 1) * P],
                        rhs=mixes[lot // PAIRS][:, carry : carry + GROUP_ROWS, :].rearrange("p k c -> p (k c)"),
                        start=start,
                        stop=not start,
                    )

                if r % 2 == 0:
                    mixed(True)
                for e, i in enumerate(MOVED):
                    group, carry = source(OFFSETS[i][0], r)
                    nc.tensor.matmul(
                        out=pixels,
                        lhsT=m_products[lot, s, e][:, group, :],
                        rhs=moves[i, carry].rearrange("p k c -> p (k c)"),
                        is_transpose=True,
                        start=e == 0 and r % 2 == 1,
                        stop=e == len(MOVED) - 1 and r % 2 == 0,
                    )
                if r % 2 == 1:
                    mixed(False)
                if place == GROUPS // 2 - 1:
                    leaving.append((lot, s, half))

            m_outs = {}

            def matrix_leave():
                lot, s, half = leaving.pop(0)
                bank = m_sums[lot, s, half]
                a, pair = divmod(lot, PAIRS)
                t = pair * PAIR + s
                if half == 0:
                    m_outs[lot, s] = m_work.tile([P, H * W], F32, name="m_out")
                result = m_outs[lot, s]
                column = t * B + LOOPED + a
                rows = slice(half * GROUPS // 2, (half + 1) * GROUPS // 2)
                nc.scalar.activation(
                    out=result.rearrange("p (k r c) -> p r k c", r=GROUPS, c=W)[:, rows],
                    in_=bank.rearrange("p (r k c) -> p r k c", k=GROUP_ROWS, c=W),
                    func=IDENTITY,
                    bias=bias[:, column : column + 1],
                    scale=1.0,
                )
                if half == 1:
                    nc.sync.dma_start(
                        out=out[LOOPED + a, t * P : (t + 1) * P].rearrange("p r w -> p (r w)"), in_=result[:]
                    )

            def matrix_turn(turn):
                messages = []
                for q in range(LOTS):
                    base = FIRST_BLOCK + 2 * GROUPS * q // BLOCKS_A_TURN
                    a, pair = divmod(q, PAIRS)
                    if pair == 0:
                        for start, per, done in ((-9, 8, 2), (3, 2, 7), (9, 1, 17))[a : a + 1]:
                            for r in range(GROUPS):
                                if turn == start + r // per:
                                    matrix_regroup(a, r)
                            if turn == done:
                                matrix_quantise(a)
                    if turn == base - 4:
                        messages = [(q, u) for u in range(GROUPS // 2)]
                first = (turn - FIRST_BLOCK) * BLOCKS_A_TURN
                for block in range(first, first + BLOCKS_A_TURN + 1):
                    if block % (GROUPS // 2) == 0:
                        for q, u in messages:
                            matrix_messages(q, u)
                        messages = []
                    if block < first + BLOCKS_A_TURN and 0 <= block < LOTS * PAIR * GROUPS:
                        matrix_block(block // (PAIR * GROUPS), block // GROUPS % PAIR, block % GROUPS)
                for q in range(LOTS):
                    for s in range(PAIR):
                        base = FIRST_BLOCK + (2 * q + s) * GROUPS // BLOCKS_A_TURN
                        for e in range(len(MOVED)):
                            if turn == base - 3 + e // 2:
                                matrix_product(q, s, e)

            def fill(b, t, k):
                bank = banks.tile([P, BANK_COLS], F32, name="bank")
                d_cols = slice(t * P, (t + 1) * P)
                words = slice(k * BAND * PITCH, k * BAND * PITCH + BANK_COLS)
                nc.tensor.matmul_mx(
                    out=bank[:],
                    lhsT=mw_codes[:, d_cols].bitcast(FP8X4),
                    lhsT_scale=mw_scales[:, d_cols],
                    rhs=x_codes[b % 2][:, words].bitcast(FP8X4),
                    rhs_scale=x_scales[b % 2][:, words],
                    start=True,
                    stop=True,
                )
                return bank[:, 0 : BANK_ROWS * PITCH].rearrange("p (r c) -> p r c", c=PITCH)

            def fills(turn):
                b, rest = divmod(turn, PAIRS * BANDS)
                pair, j = divmod(rest, BANDS)
                return [fill(b, pair * PAIR + s, j) for s in range(PAIR)]

            parts = {}

            def parts_of(turn):
                pair = turn // BANDS
                if pair not in parts:
                    parts[pair] = (
                        accs.tile([P, PAIR, H * W], F32, name="acc"),
                        sides.tile([P, PAIR, H * W], F32, name="side_a"),
                        sides.tile([P, PAIR, H * W], F32, name="side_b"),
                    )
                return parts[pair]

            def scalar_taps(turn):
                return 3 if turn >= 24 and turn % 2 == 1 else 2

            def pixels_of(turn):
                return slice(turn % BANDS * BAND * W, (turn % BANDS + 1) * BAND * W)

            def scalar_products(turn, banks_j):
                b, pair = divmod(turn // BANDS, PAIRS)
                pixels = pixels_of(turn)
                for i in reversed(range(scalar_taps(turn))):
                    bank_step, row, col = tap_window(*OFFSETS[i])
                    assert bank_step == 0
                    for s in range(PAIR):
                        column = (pair * PAIR + s) * B + b
                        nc.scalar.activation(
                            out=parts_of(turn)[i][:, s, pixels].rearrange("p (r c) -> p r c", c=W),
                            in_=banks_j[s][:, row : row + BAND, col : col + W],
                            func=IDENTITY,
                            bias=bias[:, column : column + 1] if i == 0 else 0.0,
                            scale=weight_of(i, b),
                        )

            def early_join(turn):
                if scalar_taps(turn) == 3:
                    acc, side_a, side_b = parts_of(turn)
                    pixels = pixels_of(turn)
                    nc.gpsimd.tensor_tensor(
                        out=side_a[:, :, pixels], in0=side_a[:, :, pixels], in1=side_b[:, :, pixels], op=ADD
                    )

            def vector_adds(turn, source_banks, source_step):
                b = turn // (PAIRS * BANDS)
                for i in range(scalar_taps(turn), TAPS):
                    bank_step, row, col = tap_window(*OFFSETS[i])
                    if bank_step != source_step:
                        continue
                    for s in range(PAIR):
                        band = parts_of(turn)[0][:, s, pixels_of(turn)].rearrange("p (r c) -> p r c", c=W)
                        nc.vector.scalar_tensor_tensor(
                            out=band,
                            in0=source_banks[s][:, row : row + BAND, col : col + W],
                            scalar=weight_of(i, b),
                            in1=band,
                            op0=MULT,
                            op1=ADD,
                        )

            def finish(turn, engine):
                b, pair = divmod(turn // BANDS, PAIRS)
                acc, side_a, side_b = parts_of(turn)
                pixels = pixels_of(turn)
                engine.tensor_tensor(out=acc[:, :, pixels], in0=acc[:, :, pixels], in1=side_a[:, :, pixels], op=ADD)
                j = turn % BANDS
                nc.sync.dma_start(
                    out=out[b, pair * PAIR * P : (pair + 1) * PAIR * P, j * BAND : (j + 1) * BAND, :].rearrange(
                        "(s p) r w -> p s (r w)", p=P
                    ),
                    in_=acc[:, :, pixels],
                )

            turns = LOOPED * PAIRS * BANDS
            filled = {0: fills(0)}
            scalar_products(0, filled[0])
            prepare_mw(1)
            regroup(nc.scalar.copy, 0, 5)
            load_looped(4)
            for r in range(GROUPS // 2):
                matrix_regroup_gpsimd(0, r)
            for a in range(MATRIX):
                build_mix(a)
            for turn in range(turns):
                b, step = divmod(turn, PAIRS * BANDS)
                j = turn % BANDS
                early_join(turn)
                if j > 0:
                    vector_adds(turn, filled[turn - 1], -1)
                while leaving:
                    matrix_leave()
                if turn + 1 < turns:
                    filled[turn + 1] = fills(turn + 1)
                    scalar_products(turn + 1, filled[turn + 1])
                matrix_turn(turn)
                vector_adds(turn, filled[turn], 0)
                if j > 0:
                    finish(turn, nc.gpsimd)
                if turn == 0:
                    quantise(0, (third,), 2 * third)
                    quantise_mw(1)
                    for r in range(GROUPS // 2):
                        matrix_regroup(0, GROUPS // 2 + r)
                    load_matrix(2)
                if b == 0 and step < REGROUP_STEPS:
                    regroup(nc.scalar.copy, 1, step)
                if b == 0 and step == REGROUP_STEPS - 1:
                    quantise(1)
                if b + 2 < LOOPED and step >= 2 * BANDS - EARLY:
                    regroup(nc.scalar.copy, b + 2, step - 2 * BANDS + EARLY)
                if 0 < b and b + 1 < LOOPED and step < REGROUP_STEPS - EARLY:
                    regroup(nc.scalar.copy, b + 1, step + EARLY)
                if 0 < b and b + 1 < LOOPED and step == REGROUP_STEPS - 2:
                    quantise(b + 1)
                if j == BANDS - 1:
                    vector_adds(turn - j, filled[turn], -1)
                    finish(turn - j, nc.vector if turn == turns - 1 else nc.gpsimd)
            while leaving:
                matrix_leave()
